import numpy as np
import ml_dtypes


def mxq(x, axis, fmt="e4m3"):
    dtype, down = {"e4m3": (ml_dtypes.float8_e4m3fn, 7), "e5m2": (ml_dtypes.float8_e5m2, 14)}[fmt]
    v = np.moveaxis(np.asarray(x, np.float32).astype(ml_dtypes.bfloat16).astype(np.float64), axis, -1)
    blocks = v.reshape(v.shape[:-1] + (-1, 32))
    amax = np.abs(blocks).max(-1, keepdims=True)
    byte = np.maximum(np.where(amax > 0, np.frexp(amax)[1] - 1 + 127, 0) - down, 1)
    scale = np.exp2(byte - 127.0)
    codes = (blocks / scale).astype(np.float32).astype(dtype).astype(np.float64)
    return np.moveaxis((codes * scale).reshape(v.shape), -1, axis)


WIDE = False


def mx_kscale(k):
    if not WIDE:
        return np.ones(k)
    levels = np.array([10, -10, 5, -5, 0])
    a = np.random.permutation(np.resize(levels, k // 512 * 4)).reshape(k // 512, 4)
    idx = np.arange(k)
    return np.exp2(a[idx // 512, idx % 128 // 32])


BF16 = ml_dtypes.bfloat16


def bf(x):
    return np.asarray(x, np.float32).astype(BF16)


def f64(x):
    return np.asarray(x).astype(np.float64)


E2M1 = np.array([0.0, 0.5, 1.0, 1.5, 2.0, 3.0, 4.0, 6.0, -0.0, -0.5, -1.0, -1.5, -2.0, -3.0, -4.0, -6.0])


def pack_weight(w, fmt):
    k, n = w.shape
    w = f64(bf(w)).reshape(k // 32, 32, n)
    amax = np.abs(w).max(1)
    if fmt == "e4m3":
        byte = np.frexp(amax)[1] - 1 + 127 - 7
    else:
        mant, ex = np.frexp(amax / 6.0)
        byte = np.where(mant > 0.5, ex, ex - 1) + 127
    byte = np.clip(np.where(amax > 0, byte, 1), 1, 254)
    scaled = (w * np.exp2(127.0 - byte)[:, None, :]).reshape(k, n).astype(np.float32)
    by_word = np.ascontiguousarray(scaled.reshape(k // 512, 128, 4, n).transpose(0, 1, 3, 2))
    if fmt == "e4m3":
        words = by_word.astype(ml_dtypes.float8_e4m3fn).view(np.uint8)
    else:
        c = by_word.astype(ml_dtypes.float4_e2m1fn).view(np.uint8) & 0xF
        words = c[..., 0::2] | (c[..., 1::2] << 4)
    return np.ascontiguousarray(words), np.ascontiguousarray(byte.astype(np.uint8).reshape(k // 512, 16, n))


def unpack_weight(words, scales, fmt):
    g, p, n, _ = words.shape
    if fmt == "e4m3":
        vals = np.ascontiguousarray(words).view(ml_dtypes.float8_e4m3fn).astype(np.float64)
    else:
        nib = np.empty((g, p, n, 4), np.uint8)
        nib[..., 0::2] = words & 0xF
        nib[..., 1::2] = words >> 4
        vals = E2M1[nib]
    vals = vals * np.repeat(np.exp2(scales.astype(np.float64) - 127.0), 8, axis=1)[..., None]
    return vals.transpose(0, 1, 3, 2).reshape(g * 512, n)

def pack4(w):
    words, scales = pack_weight(w, "e2m1")
    return words.reshape(words.shape[0], 128, -1), scales


def unpack4(words, scales):
    return unpack_weight(words.reshape(words.shape[0], 128, -1, 2), scales, "e2m1")


B, IN, H, OUT, L, STEPS = 1024, 512, 1024, 128, 3, 3
LN_EPS = 1e-5


def layer_norm(v, g, b):
    m = v.mean(-1, keepdims=True)
    var = ((v - m) ** 2).mean(-1, keepdims=True)
    return (v - m) / np.sqrt(var + LN_EPS) * g + b


def setup_inputs():
    s = mx_kscale(H)
    s = s / s.max()
    h = bf(np.random.standard_normal((B, H)) * s)
    stack = (np.random.standard_normal((L, H, H)) / np.sqrt(H) / s).swapaxes(1, 2)
    words, scales = pack4(stack.reshape(-1, H))
    return {"h": h,
            "W_liq_words": words,
            "W_liq_scales": scales,
            "b_liq": bf(np.random.standard_normal((L, H)) * 0.3),
            "g_liq": bf(1.0 + 0.1 * np.random.standard_normal((L, H))),
            "beta_liq": bf(np.random.standard_normal((L, H)) * 0.3)}


def reference(h, W_liq_words, W_liq_scales, b_liq, g_liq, beta_liq):
    h = f64(h)
    lin = mxq(h, 1, "e4m3") @ unpack4(W_liq_words, W_liq_scales).reshape(L, H, H)
    pre = h[None] + lin + f64(b_liq)[:, None, :]
    return layer_norm(pre, f64(g_liq)[:, None, :], f64(beta_liq)[:, None, :]).sum(0)

@@ -1,0 +1,174 @@
+from contextlib import ExitStack
+
+import concourse.mybir as mybir
+from concourse.masks import make_identity
+
+F32 = mybir.dt.float32
+BF16 = mybir.dt.bfloat16
+I32 = mybir.dt.int32
+U32 = mybir.dt.uint32
+U8 = mybir.dt.uint8
+FP8X4 = mybir.dt.float8_e4m3fn_x4
+FP4X4 = mybir.dt.float4_e2m1fn_x4
+ALU = mybir.AluOpType
+ACT = mybir.ActivationFunctionType
+
+P = 128
+ROWS = 1024
+H = 1024
+BRANCHES = 3
+LN_EPS = 1e-5
+K_PASS = 4 * P
+PASSES = H // K_PASS
+ROW_TILES = ROWS // P
+BANK = 512
+HALVES = H // BANK
+
+FLOPS = 2 * BRANCHES * ROWS * H * H
+
+
+def tile_advancedliquidneuralnetwork_pa_e_kernel(
+    tc, h, W_liq_words, W_liq_scales, b_liq, g_liq, beta_liq, out
+):
+    nc = tc.nc
+    with ExitStack() as ctx:
+        keep = ctx.enter_context(tc.tile_pool(name="keep", bufs=1))
+        stage = ctx.enter_context(tc.tile_pool(name="stage", bufs=2))
+        shifted = ctx.enter_context(tc.tile_pool(name="shifted", bufs=4))
+        work = ctx.enter_context(tc.tile_pool(name="work", bufs=3))
+        stats = ctx.enter_context(tc.tile_pool(name="stats", bufs=6))
+        turn_psum = ctx.enter_context(tc.psum_pool(name="turn_psum", bufs=2))
+        lin_psum = ctx.enter_context(tc.psum_pool(name="lin_psum", bufs=2))
+
+        h_sb = keep.tile([P, ROW_TILES, H], BF16)
+        w_words = keep.tile([P, BRANCHES * PASSES, 2 * H], U8, align_bytes=64)
+        w_scales = keep.tile([P, BRANCHES * PASSES, H], U8, align_bytes=64)
+        nc.vector.memset(w_scales[:].bitcast(I32), 0)
+
+        nc.sync.dma_start(out=h_sb[:, 0, :], in_=h[0:P, :])
+        for quad in range(4):
+            nc.sync.dma_start(
+                out=w_scales[32 * quad : 32 * quad + 4, :, :].bitcast(I32),
+                in_=W_liq_scales[:, 4 * quad : 4 * quad + 4, :].rearrange("c r n -> r c n").bitcast(I32),
+            )
+        for c in range(BRANCHES * PASSES):
+            nc.sync.dma_start(out=w_words[:, c, :].bitcast(I32), in_=W_liq_words[c].bitcast(I32))
+        for rt in range(1, ROW_TILES):
+            nc.sync.dma_start(out=h_sb[:, rt, :], in_=h[rt * P : (rt + 1) * P, :])
+
+        b_all = keep.tile([P, BRANCHES, H], BF16)
+        g_all = keep.tile([P, BRANCHES, H], BF16)
+        beta_all = keep.tile([P, BRANCHES, H], BF16)
+        for repeated, vectors in ((b_all, b_liq), (g_all, g_liq), (beta_all, beta_liq)):
+            nc.scalar.dma_start(
+                out=repeated[:].rearrange("p l n -> p (l n)"),
+                in_=vectors.rearrange("l n -> (l n)").partition_broadcast(P),
+            )
+        beta_sum = keep.tile([P, H], F32)
+        nc.vector.tensor_tensor(out=beta_sum[:], in0=beta_all[:, 0, :], in1=beta_all[:, 1, :], op=ALU.add)
+        nc.vector.tensor_tensor(out=beta_sum[:], in0=beta_sum[:], in1=beta_all[:, 2, :], op=ALU.add)
+
+        identity = keep.tile([P, P], F32)
+        make_identity(nc, identity[:])
+        eps = keep.tile([P, 1], F32)
+        nc.vector.memset(eps[:], LN_EPS)
+
+        h_codes = keep.tile([P, ROW_TILES, PASSES * P], U32, align_bytes=64)
+        h_scales = keep.tile([P, ROW_TILES, PASSES * P], U8, align_bytes=64)
+
+        for rt in range(ROW_TILES):
+            pairs = h_sb[:, rt, :].bitcast(F32)
+            turned = turn_psum.tile([P, PASSES, 2, P], F32)
+            for c in range(PASSES):
+                for u in range(2):
+                    nc.tensor.transpose(
+                        turned[:, c, u, :], pairs[:, 256 * c + u : 256 * (c + 1) : 2], identity[:]
+                    )
+            grouped = stage.tile([P, PASSES, P, 2], F32, align_bytes=64)
+            nc.vector.tensor_copy(out=grouped[:], in_=turned[:].rearrange("p c u r -> p c r u"))
+            nc.vector.quantize_mx(
+                out=h_codes[:, rt, :].bitcast(FP8X4),
+                scales=h_scales[:, rt, :],
+                in_=grouped[:].rearrange("p c r u -> p (c r u)").bitcast(BF16),
+            )
+
+            total = work.tile([P, H], F32)
+            for l in range(BRANCHES):
+                h_plus_b = shifted.tile([P, H], F32)
+                nc.gpsimd.tensor_tensor(
+                    out=h_plus_b[:], in0=h_sb[:, rt, :], in1=b_all[:, l, :], op=ALU.add
+                )
+
+                lin = lin_psum.tile([P, HALVES, BANK], F32)
+                for half in range(HALVES):
+                    for c in range(PASSES):
+                        chunk = l * PASSES + c
+                        nc.tensor.matmul_mx(
+                            out=lin[:, half, :],
+                            lhsT=h_codes[:, rt, c * P : (c + 1) * P].bitcast(FP8X4),
+                            lhsT_scale=h_scales[:, rt, c * P : (c + 1) * P],
+                            rhs=w_words[:, chunk, 2 * BANK * half : 2 * BANK * (half + 1)].bitcast(FP4X4),
+                            rhs_scale=w_scales[:, chunk, BANK * half : BANK * (half + 1)],
+                            start=(c == 0),
+                            stop=(c == PASSES - 1),
+                        )
+
+                pre = work.tile([P, H], F32)
+                row_sums = stats.tile([P, HALVES], F32)
+                for half in range(HALVES):
+                    cols = slice(BANK * half, BANK * (half + 1))
+                    nc.vector.scalar_tensor_tensor(
+                        out=pre[:, cols],
+                        in0=lin[:, half, :],
+                        scalar=1.0,
+                        in1=h_plus_b[:, cols],
+                        op0=ALU.mult,
+                        op1=ALU.add,
+                        accum_out=row_sums[:, half : half + 1],
+                    )
+                neg_mean = stats.tile([P, 1], F32)
+                nc.vector.tensor_scalar(
+                    out=neg_mean[:],
+                    in0=row_sums[:, 0:1],
+                    scalar1=row_sums[:, 1:2],
+                    scalar2=-1.0 / H,
+                    op0=ALU.add,
+                    op1=ALU.mult,
+                )
+
+                squares = stage.tile([P, H], BF16)
+                sum_squares = stats.tile([P, 1], F32)
+                nc.scalar.activation(
+                    out=squares[:],
+                    in_=pre[:],
+                    func=ACT.Square,
+                    bias=neg_mean[:],
+                    scale=1.0,
+                    accum_out=sum_squares[:],
+                )
+                std = stats.tile([P, 1], F32)
+                nc.scalar.activation(
+                    out=std[:], in_=sum_squares[:], func=ACT.Sqrt, bias=eps[:], scale=1.0 / H
+                )
+                inv_std = stats.tile([P, 1], F32)
+                nc.vector.reciprocal(out=inv_std[:], in_=std[:])
+
+                gained = work.tile([P, H], F32)
+                nc.vector.scalar_tensor_tensor(
+                    out=gained[:],
+                    in0=pre[:],
+                    scalar=neg_mean[:],
+                    in1=g_all[:, l, :],
+                    op0=ALU.add,
+                    op1=ALU.mult,
+                )
+                nc.vector.scalar_tensor_tensor(
+                    out=total[:],
+                    in0=gained[:],
+                    scalar=inv_std[:],
+                    in1=(beta_sum[:] if l == 0 else total[:]),
+                    op0=ALU.mult,
+                    op1=ALU.add,
+                )
+
+            nc.sync.dma_start(out=out[rt * P : (rt + 1) * P, :], in_=total[:])

@@ -95,7 +95,7 @@ def tile_advancedliquidneuralnetwork_pa_e_kernel(
             total = work.tile([P, H], F32)
             for l in range(BRANCHES):
                 h_plus_b = shifted.tile([P, H], F32)
-                nc.gpsimd.tensor_tensor(
+                nc.vector.tensor_tensor(
                     out=h_plus_b[:], in0=h_sb[:, rt, :], in1=b_all[:, l, :], op=ALU.add
                 )
 

@@ -20,11 +20,19 @@ BRANCHES = 3
 LN_EPS = 1e-5
 K_PASS = 4 * P
 PASSES = H // K_PASS
-ROW_TILES = ROWS // P
 BANK = 512
+GROUP_TILES = BANK // P
+GROUPS = ROWS // BANK
+FEATURE_TILES = H // P
 HALVES = H // BANK
+BLOCKS = GROUPS * BRANCHES
+STEPS = GROUP_TILES
 
 FLOPS = 2 * BRANCHES * ROWS * H * H
+
+LAG_ROWS = STEPS
+LAG_NORMALISE = 1
+LAG_BACK = STEPS
 
 
 def tile_advancedliquidneuralnetwork_pa_e_kernel(
@@ -33,142 +41,237 @@ def tile_advancedliquidneuralnetwork_pa_e_kernel(
     nc = tc.nc
     with ExitStack() as ctx:
         keep = ctx.enter_context(tc.tile_pool(name="keep", bufs=1))
-        stage = ctx.enter_context(tc.tile_pool(name="stage", bufs=2))
-        shifted = ctx.enter_context(tc.tile_pool(name="shifted", bufs=4))
-        work = ctx.enter_context(tc.tile_pool(name="work", bufs=3))
-        stats = ctx.enter_context(tc.tile_pool(name="stats", bufs=6))
-        turn_psum = ctx.enter_context(tc.psum_pool(name="turn_psum", bufs=2))
+        blocks = ctx.enter_context(tc.tile_pool(name="blocks", bufs=2))
+        stats = ctx.enter_context(tc.tile_pool(name="stats", bufs=8))
         lin_psum = ctx.enter_context(tc.psum_pool(name="lin_psum", bufs=2))
+        rows_psum = ctx.enter_context(tc.psum_pool(name="rows_psum", bufs=2))
+        back_psum = ctx.enter_context(tc.psum_pool(name="back_psum", bufs=2))
+        out_psum = ctx.enter_context(tc.psum_pool(name="out_psum", bufs=2))
+        ctx.enter_context(tc.manual_schedule())
 
-        h_sb = keep.tile([P, ROW_TILES, H], BF16)
+        h_sb = keep.tile([P, GROUPS * GROUP_TILES, H], BF16)
         w_words = keep.tile([P, BRANCHES * PASSES, 2 * H], U8, align_bytes=64)
         w_scales = keep.tile([P, BRANCHES * PASSES, H], U8, align_bytes=64)
         nc.vector.memset(w_scales[:].bitcast(I32), 0)
+        vector_rows = keep.tile([P, P], BF16)
+        nc.vector.memset(vector_rows[:], 0.0)
 
-        nc.sync.dma_start(out=h_sb[:, 0, :], in_=h[0:P, :])
+        for rt in range(GROUP_TILES):
+            nc.sync.dma_start(out=h_sb[:, rt, :], in_=h[rt * P : (rt + 1) * P, :])
         for quad in range(4):
             nc.sync.dma_start(
                 out=w_scales[32 * quad : 32 * quad + 4, :, :].bitcast(I32),
                 in_=W_liq_scales[:, 4 * quad : 4 * quad + 4, :].rearrange("c r n -> r c n").bitcast(I32),
             )
-        for c in range(BRANCHES * PASSES):
-            nc.sync.dma_start(out=w_words[:, c, :].bitcast(I32), in_=W_liq_words[c].bitcast(I32))
-        for rt in range(1, ROW_TILES):
+        for chunk in range(BRANCHES * PASSES):
+            nc.sync.dma_start(out=w_words[:, chunk, :].bitcast(I32), in_=W_liq_words[chunk].bitcast(I32))
+        for rt in range(GROUP_TILES, GROUPS * GROUP_TILES):
             nc.sync.dma_start(out=h_sb[:, rt, :], in_=h[rt * P : (rt + 1) * P, :])
-
-        b_all = keep.tile([P, BRANCHES, H], BF16)
-        g_all = keep.tile([P, BRANCHES, H], BF16)
-        beta_all = keep.tile([P, BRANCHES, H], BF16)
-        for repeated, vectors in ((b_all, b_liq), (g_all, g_liq), (beta_all, beta_liq)):
+        for kind, vectors in enumerate((b_liq, g_liq, beta_liq)):
             nc.scalar.dma_start(
-                out=repeated[:].rearrange("p l n -> p (l n)"),
-                in_=vectors.rearrange("l n -> (l n)").partition_broadcast(P),
+                out=vector_rows[32 * kind : 32 * kind + BRANCHES * FEATURE_TILES, :],
+                in_=vectors.rearrange("l (ft p) -> (l ft) p", p=P),
             )
-        beta_sum = keep.tile([P, H], F32)
-        nc.vector.tensor_tensor(out=beta_sum[:], in0=beta_all[:, 0, :], in1=beta_all[:, 1, :], op=ALU.add)
-        nc.vector.tensor_tensor(out=beta_sum[:], in0=beta_sum[:], in1=beta_all[:, 2, :], op=ALU.add)
 
         identity = keep.tile([P, P], F32)
         make_identity(nc, identity[:])
         eps = keep.tile([P, 1], F32)
         nc.vector.memset(eps[:], LN_EPS)
 
-        h_codes = keep.tile([P, ROW_TILES, PASSES * P], U32, align_bytes=64)
-        h_scales = keep.tile([P, ROW_TILES, PASSES * P], U8, align_bytes=64)
+        h_codes = keep.tile([P, GROUPS, PASSES, BANK], U32, align_bytes=64)
+        h_scales = keep.tile([P, GROUPS, PASSES, BANK], U8, align_bytes=64)
 
-        for rt in range(ROW_TILES):
-            pairs = h_sb[:, rt, :].bitcast(F32)
-            turned = turn_psum.tile([P, PASSES, 2, P], F32)
-            for c in range(PASSES):
-                for u in range(2):
-                    nc.tensor.transpose(
-                        turned[:, c, u, :], pairs[:, 256 * c + u : 256 * (c + 1) : 2], identity[:]
-                    )
-            grouped = stage.tile([P, PASSES, P, 2], F32, align_bytes=64)
-            nc.vector.tensor_copy(out=grouped[:], in_=turned[:].rearrange("p c u r -> p c r u"))
-            nc.vector.quantize_mx(
-                out=h_codes[:, rt, :].bitcast(FP8X4),
-                scales=h_scales[:, rt, :],
-                in_=grouped[:].rearrange("p c r u -> p (c r u)").bitcast(BF16),
-            )
-
-            total = work.tile([P, H], F32)
-            for l in range(BRANCHES):
-                h_plus_b = shifted.tile([P, H], F32)
-                nc.vector.tensor_tensor(
-                    out=h_plus_b[:], in0=h_sb[:, rt, :], in1=b_all[:, l, :], op=ALU.add
-                )
-
-                lin = lin_psum.tile([P, HALVES, BANK], F32)
-                for half in range(HALVES):
-                    for c in range(PASSES):
-                        chunk = l * PASSES + c
-                        nc.tensor.matmul_mx(
-                            out=lin[:, half, :],
-                            lhsT=h_codes[:, rt, c * P : (c + 1) * P].bitcast(FP8X4),
-                            lhsT_scale=h_scales[:, rt, c * P : (c + 1) * P],
-                            rhs=w_words[:, chunk, 2 * BANK * half : 2 * BANK * (half + 1)].bitcast(FP4X4),
-                            rhs_scale=w_scales[:, chunk, BANK * half : BANK * (half + 1)],
-                            start=(c == 0),
-                            stop=(c == PASSES - 1),
+        def quantise_group(grp):
+            grouped = blocks.tile([P, PASSES, BANK, 2], F32, align_bytes=64, name="grouped")
+            for r4 in range(GROUP_TILES):
+                pairs = h_sb[:, GROUP_TILES * grp + r4, :].bitcast(F32)
+                turned = rows_psum.tile([P, PASSES, 2, P], F32, tag="y_rows", name="turned")
+                for c in range(PASSES):
+                    for u in range(2):
+                        nc.tensor.transpose(
+                            turned[:, c, u, :], pairs[:, 256 * c + u : 256 * (c + 1) : 2], identity[:]
                         )
+                side_by_side = grouped[:, :, P * r4 : P * (r4 + 1), :]
+                if r4 % 2 == 0:
+                    nc.vector.tensor_copy(out=side_by_side, in_=turned[:].rearrange("p c u r -> p c r u"))
+                else:
+                    nc.scalar.copy(out=side_by_side, in_=turned[:].rearrange("p c u r -> p c r u"))
+            for c in range(PASSES):
+                nc.vector.quantize_mx(
+                    out=h_codes[:, grp, c, :].bitcast(FP8X4),
+                    scales=h_scales[:, grp, c, :],
+                    in_=grouped[:, c, :, :].rearrange("p r u -> p (r u)").bitcast(BF16),
+                )
 
-                pre = work.tile([P, H], F32)
-                row_sums = stats.tile([P, HALVES], F32)
-                for half in range(HALVES):
-                    cols = slice(BANK * half, BANK * (half + 1))
-                    nc.vector.scalar_tensor_tensor(
-                        out=pre[:, cols],
-                        in0=lin[:, half, :],
-                        scalar=1.0,
-                        in1=h_plus_b[:, cols],
-                        op0=ALU.mult,
-                        op1=ALU.add,
-                        accum_out=row_sums[:, half : half + 1],
+        quantise_group(0)
+
+        vector_rows_f32 = keep.tile([P, P], F32)
+        nc.vector.tensor_copy(out=vector_rows_f32[:], in_=vector_rows[:])
+        vector_bank = out_psum.tile([P, P], F32, tag="out_rows")
+        nc.tensor.transpose(vector_bank[:], vector_rows_f32[:], identity[:])
+        vector_columns = keep.tile([P, P], F32)
+        nc.vector.tensor_copy(out=vector_columns[:], in_=vector_bank[:])
+
+        def column(kind, l, ft):
+            at = 32 * kind + FEATURE_TILES * l + ft
+            return vector_columns[:, at : at + 1]
+
+        beta_sum = keep.tile([P, FEATURE_TILES], F32)
+        nc.vector.tensor_tensor(
+            out=beta_sum[:], in0=vector_columns[:, 64:72], in1=vector_columns[:, 72:80], op=ALU.add
+        )
+        nc.vector.tensor_tensor(out=beta_sum[:], in0=beta_sum[:], in1=vector_columns[:, 80:88], op=ALU.add)
+
+        y_feat = {}
+        pre_rows = {}
+        z_rows = {}
+        total_feat = {}
+        neg_mean = {}
+        inv_std = {}
+
+        def product(block, step):
+            grp, l = divmod(block, BRANCHES)
+            if step == 0:
+                y_feat[block] = blocks.tile([P, FEATURE_TILES, BANK], F32, name="y_feat")
+            for ft in (2 * step, 2 * step + 1):
+                lin = lin_psum.tile([P, BANK], F32, name="lin")
+                for c in range(PASSES):
+                    chunk = l * PASSES + c
+                    nc.tensor.matmul_mx(
+                        out=lin[:],
+                        lhsT=w_words[:, chunk, 2 * P * ft : 2 * P * (ft + 1)].bitcast(FP4X4),
+                        lhsT_scale=w_scales[:, chunk, P * ft : P * (ft + 1)],
+                        rhs=h_codes[:, grp, c, :].bitcast(FP8X4),
+                        rhs_scale=h_scales[:, grp, c, :],
+                        start=(c == 0),
+                        stop=(c == PASSES - 1),
                     )
-                neg_mean = stats.tile([P, 1], F32)
-                nc.vector.tensor_scalar(
-                    out=neg_mean[:],
-                    in0=row_sums[:, 0:1],
-                    scalar1=row_sums[:, 1:2],
-                    scalar2=-1.0 / H,
-                    op0=ALU.add,
-                    op1=ALU.mult,
+                nc.scalar.activation(
+                    out=y_feat[block][:, ft, :], in_=lin[:], func=ACT.Identity, bias=column(0, l, ft), scale=1.0
                 )
 
-                squares = stage.tile([P, H], BF16)
-                sum_squares = stats.tile([P, 1], F32)
-                nc.scalar.activation(
-                    out=squares[:],
-                    in_=pre[:],
-                    func=ACT.Square,
-                    bias=neg_mean[:],
-                    scale=1.0,
-                    accum_out=sum_squares[:],
-                )
-                std = stats.tile([P, 1], F32)
-                nc.scalar.activation(
-                    out=std[:], in_=sum_squares[:], func=ACT.Sqrt, bias=eps[:], scale=1.0 / H
-                )
-                inv_std = stats.tile([P, 1], F32)
-                nc.vector.reciprocal(out=inv_std[:], in_=std[:])
-
-                gained = work.tile([P, H], F32)
+        def to_rows(block, r4):
+            grp, l = divmod(block, BRANCHES)
+            unit = (block, r4)
+            if r4 == 0:
+                pre_rows[block] = blocks.tile([P, GROUP_TILES, H], F32, name="pre_rows")
+            row_sums = stats.tile([P, HALVES], F32, name="row_sums")
+            for half in range(HALVES):
+                y_rows = rows_psum.tile([P, BANK], F32, name="y_rows")
+                for q in range(BANK // P):
+                    nc.tensor.transpose(
+                        y_rows[:, P * q : P * (q + 1)],
+                        y_feat[block][:, (BANK // P) * half + q, P * r4 : P * (r4 + 1)],
+                        identity[:],
+                    )
+                cols = slice(BANK * half, BANK * (half + 1))
                 nc.vector.scalar_tensor_tensor(
-                    out=gained[:],
-                    in0=pre[:],
-                    scalar=neg_mean[:],
-                    in1=g_all[:, l, :],
-                    op0=ALU.add,
-                    op1=ALU.mult,
-                )
-                nc.vector.scalar_tensor_tensor(
-                    out=total[:],
-                    in0=gained[:],
-                    scalar=inv_std[:],
-                    in1=(beta_sum[:] if l == 0 else total[:]),
+                    out=pre_rows[block][:, r4, cols],
+                    in0=y_rows[:],
+                    scalar=1.0,
+                    in1=h_sb[:, GROUP_TILES * grp + r4, cols],
                     op0=ALU.mult,
                     op1=ALU.add,
+                    accum_out=row_sums[:, half : half + 1],
                 )
+            neg_mean[unit] = stats.tile([P, 1], F32, name="neg_mean")
+            nc.vector.tensor_scalar(
+                out=neg_mean[unit][:],
+                in0=row_sums[:, 0:1],
+                scalar1=row_sums[:, 1:2],
+                scalar2=-1.0 / H,
+                op0=ALU.add,
+                op1=ALU.mult,
+            )
+            squares = blocks.tile([P, H], BF16, name="squares")
+            sum_squares = stats.tile([P, 1], F32, name="sum_squares")
+            nc.scalar.activation(
+                out=squares[:],
+                in_=pre_rows[block][:, r4, :],
+                func=ACT.Square,
+                bias=neg_mean[unit][:],
+                scale=1.0,
+                accum_out=sum_squares[:],
+            )
+            inv_std[unit] = stats.tile([P, 1], F32, name="inv_std")
+            nc.scalar.activation(
+                out=inv_std[unit][:], in_=sum_squares[:], func=ACT.Abs_reciprocal_sqrt, bias=eps[:], scale=1.0 / H
+            )
 
-            nc.sync.dma_start(out=out[rt * P : (rt + 1) * P, :], in_=total[:])
+        def normalise(block, r4):
+            unit = (block, r4)
+            if r4 == 0:
+                z_rows[block] = blocks.tile([P, GROUP_TILES, H], F32, name="z_rows")
+            nc.vector.tensor_scalar(
+                out=z_rows[block][:, r4, :],
+                in0=pre_rows[block][:, r4, :],
+                scalar1=neg_mean[unit][:],
+                scalar2=inv_std[unit][:],
+                op0=ALU.add,
+                op1=ALU.mult,
+            )
+
+        def gain_and_add(block, step):
+            grp, l = divmod(block, BRANCHES)
+            if l == 0 and step == 0:
+                total_feat[grp] = blocks.tile([P, FEATURE_TILES, BANK], F32, name="total_feat")
+            for ft in (2 * step, 2 * step + 1):
+                z_feat = back_psum.tile([P, BANK], F32, name="z_feat")
+                for r4 in range(GROUP_TILES):
+                    nc.tensor.transpose(
+                        z_feat[:, P * r4 : P * (r4 + 1)], z_rows[block][:, r4, P * ft : P * (ft + 1)], identity[:]
+                    )
+                if l == 0:
+                    nc.scalar.activation(
+                        out=total_feat[grp][:, ft, :],
+                        in_=z_feat[:],
+                        func=ACT.Identity,
+                        bias=beta_sum[:, ft : ft + 1],
+                        scale=column(1, l, ft),
+                    )
+                else:
+                    nc.vector.scalar_tensor_tensor(
+                        out=total_feat[grp][:, ft, :],
+                        in0=z_feat[:],
+                        scalar=column(1, l, ft),
+                        in1=total_feat[grp][:, ft, :],
+                        op0=ALU.mult,
+                        op1=ALU.add,
+                    )
+
+        def finish(grp, r4):
+            result = blocks.tile([P, H], F32, name="result")
+            for half in range(HALVES):
+                out_rows = out_psum.tile([P, BANK], F32, name="out_rows")
+                for q in range(BANK // P):
+                    nc.tensor.transpose(
+                        out_rows[:, P * q : P * (q + 1)],
+                        total_feat[grp][:, (BANK // P) * half + q, P * r4 : P * (r4 + 1)],
+                        identity[:],
+                    )
+                cols = slice(BANK * half, BANK * (half + 1))
+                if half == 0:
+                    nc.scalar.copy(out=result[:, cols], in_=out_rows[:])
+                else:
+                    nc.vector.tensor_copy(out=result[:, cols], in_=out_rows[:])
+            rt = GROUP_TILES * grp + r4
+            nc.sync.dma_start(out=out[rt * P : (rt + 1) * P, :], in_=result[:])
+
+        rows_at = LAG_ROWS
+        normalise_at = rows_at + LAG_NORMALISE
+        back_at = normalise_at + LAG_BACK
+        all_steps = BLOCKS * STEPS
+        for now in range(all_steps + back_at + STEPS):
+            if now < all_steps:
+                product(*divmod(now, STEPS))
+            if now == STEPS:
+                quantise_group(1)
+            if 0 <= now - rows_at < all_steps:
+                to_rows(*divmod(now - rows_at, STEPS))
+            if 0 <= now - back_at < all_steps:
+                gain_and_add(*divmod(now - back_at, STEPS))
+            if 0 <= now - normalise_at < all_steps:
+                normalise(*divmod(now - normalise_at, STEPS))
+            block, r4 = divmod(now - back_at, STEPS)
+            if block > 0 and block % BRANCHES == 0:
+                finish(block // BRANCHES - 1, r4)

@@ -27,10 +27,11 @@ FEATURE_TILES = H // P
 HALVES = H // BANK
 BLOCKS = GROUPS * BRANCHES
 STEPS = GROUP_TILES
+ROW_TILES = GROUPS * GROUP_TILES
 
 FLOPS = 2 * BRANCHES * ROWS * H * H
 
-LAG_ROWS = STEPS
+LAG_PRODUCT = 2
 LAG_NORMALISE = 1
 LAG_BACK = STEPS
 
@@ -42,134 +43,110 @@ def tile_advancedliquidneuralnetwork_pa_e_kernel(
     with ExitStack() as ctx:
         keep = ctx.enter_context(tc.tile_pool(name="keep", bufs=1))
         blocks = ctx.enter_context(tc.tile_pool(name="blocks", bufs=2))
+        units = ctx.enter_context(tc.tile_pool(name="units", bufs=4))
         stats = ctx.enter_context(tc.tile_pool(name="stats", bufs=8))
         lin_psum = ctx.enter_context(tc.psum_pool(name="lin_psum", bufs=2))
-        rows_psum = ctx.enter_context(tc.psum_pool(name="rows_psum", bufs=2))
         back_psum = ctx.enter_context(tc.psum_pool(name="back_psum", bufs=2))
         out_psum = ctx.enter_context(tc.psum_pool(name="out_psum", bufs=2))
         ctx.enter_context(tc.manual_schedule())
 
-        h_sb = keep.tile([P, GROUPS * GROUP_TILES, H], BF16)
+        h_sb = keep.tile([P, ROW_TILES, H], BF16)
         w_words = keep.tile([P, BRANCHES * PASSES, 2 * H], U8, align_bytes=64)
         w_scales = keep.tile([P, BRANCHES * PASSES, H], U8, align_bytes=64)
         nc.vector.memset(w_scales[:].bitcast(I32), 0)
         vector_rows = keep.tile([P, P], BF16)
         nc.vector.memset(vector_rows[:], 0.0)
+        b_all = keep.tile([P, BRANCHES, H], BF16)
 
-        for rt in range(GROUP_TILES):
-            nc.sync.dma_start(out=h_sb[:, rt, :], in_=h[rt * P : (rt + 1) * P, :])
+        nc.sync.dma_start(out=h_sb[:, 0, :], in_=h[0:P, :])
         for quad in range(4):
             nc.sync.dma_start(
                 out=w_scales[32 * quad : 32 * quad + 4, :, :].bitcast(I32),
                 in_=W_liq_scales[:, 4 * quad : 4 * quad + 4, :].rearrange("c r n -> r c n").bitcast(I32),
             )
-        for chunk in range(BRANCHES * PASSES):
+        for chunk in range(PASSES):
             nc.sync.dma_start(out=w_words[:, chunk, :].bitcast(I32), in_=W_liq_words[chunk].bitcast(I32))
-        for rt in range(GROUP_TILES, GROUPS * GROUP_TILES):
+        for rt in range(1, GROUP_TILES):
             nc.sync.dma_start(out=h_sb[:, rt, :], in_=h[rt * P : (rt + 1) * P, :])
-        for kind, vectors in enumerate((b_liq, g_liq, beta_liq)):
+        for chunk in range(PASSES, BRANCHES * PASSES):
+            nc.sync.dma_start(out=w_words[:, chunk, :].bitcast(I32), in_=W_liq_words[chunk].bitcast(I32))
+        for rt in range(GROUP_TILES, ROW_TILES):
+            nc.sync.dma_start(out=h_sb[:, rt, :], in_=h[rt * P : (rt + 1) * P, :])
+        for kind, vectors in enumerate((g_liq, beta_liq)):
             nc.scalar.dma_start(
                 out=vector_rows[32 * kind : 32 * kind + BRANCHES * FEATURE_TILES, :],
                 in_=vectors.rearrange("l (ft p) -> (l ft) p", p=P),
             )
+        for l in range(BRANCHES):
+            nc.scalar.dma_start(out=b_all[:, l, :], in_=b_liq[l].partition_broadcast(P))
 
         identity = keep.tile([P, P], F32)
         make_identity(nc, identity[:])
         eps = keep.tile([P, 1], F32)
         nc.vector.memset(eps[:], LN_EPS)
 
-        h_codes = keep.tile([P, GROUPS, PASSES, BANK], U32, align_bytes=64)
-        h_scales = keep.tile([P, GROUPS, PASSES, BANK], U8, align_bytes=64)
+        h_codes = keep.tile([P, ROW_TILES, PASSES * P], U32, align_bytes=64)
+        h_scales = keep.tile([P, ROW_TILES, PASSES * P], U8, align_bytes=64)
 
-        def quantise_group(grp):
-            grouped = blocks.tile([P, PASSES, BANK, 2], F32, align_bytes=64, name="grouped")
-            for r4 in range(GROUP_TILES):
-                pairs = h_sb[:, GROUP_TILES * grp + r4, :].bitcast(F32)
-                turned = rows_psum.tile([P, PASSES, 2, P], F32, tag="y_rows", name="turned")
-                for c in range(PASSES):
-                    for u in range(2):
-                        nc.tensor.transpose(
-                            turned[:, c, u, :], pairs[:, 256 * c + u : 256 * (c + 1) : 2], identity[:]
-                        )
-                side_by_side = grouped[:, :, P * r4 : P * (r4 + 1), :]
-                if r4 % 2 == 0:
-                    nc.vector.tensor_copy(out=side_by_side, in_=turned[:].rearrange("p c u r -> p c r u"))
-                else:
-                    nc.scalar.copy(out=side_by_side, in_=turned[:].rearrange("p c u r -> p c r u"))
+        def quantise_row_tile(rt):
+            pairs = h_sb[:, rt, :].bitcast(F32)
+            turned = out_psum.tile([P, PASSES, 2, P], F32, tag="out_rows", name="turned")
             for c in range(PASSES):
-                nc.vector.quantize_mx(
-                    out=h_codes[:, grp, c, :].bitcast(FP8X4),
-                    scales=h_scales[:, grp, c, :],
-                    in_=grouped[:, c, :, :].rearrange("p r u -> p (r u)").bitcast(BF16),
-                )
+                for u in range(2):
+                    nc.tensor.transpose(
+                        turned[:, c, u, :], pairs[:, 256 * c + u : 256 * (c + 1) : 2], identity[:]
+                    )
+            grouped = blocks.tile([P, PASSES, P, 2], F32, align_bytes=64, name="grouped")
+            nc.vector.tensor_copy(out=grouped[:], in_=turned[:].rearrange("p c u r -> p c r u"))
+            nc.vector.quantize_mx(
+                out=h_codes[:, rt, :].bitcast(FP8X4),
+                scales=h_scales[:, rt, :],
+                in_=grouped[:].rearrange("p c r u -> p (c r u)").bitcast(BF16),
+            )
 
-        quantise_group(0)
-
-        vector_rows_f32 = keep.tile([P, P], F32)
-        nc.vector.tensor_copy(out=vector_rows_f32[:], in_=vector_rows[:])
-        vector_bank = out_psum.tile([P, P], F32, tag="out_rows")
-        nc.tensor.transpose(vector_bank[:], vector_rows_f32[:], identity[:])
-        vector_columns = keep.tile([P, P], F32)
-        nc.vector.tensor_copy(out=vector_columns[:], in_=vector_bank[:])
-
-        def column(kind, l, ft):
-            at = 32 * kind + FEATURE_TILES * l + ft
-            return vector_columns[:, at : at + 1]
-
-        beta_sum = keep.tile([P, FEATURE_TILES], F32)
-        nc.vector.tensor_tensor(
-            out=beta_sum[:], in0=vector_columns[:, 64:72], in1=vector_columns[:, 72:80], op=ALU.add
-        )
-        nc.vector.tensor_tensor(out=beta_sum[:], in0=beta_sum[:], in1=vector_columns[:, 80:88], op=ALU.add)
-
-        y_feat = {}
+        h_plus_b = {}
         pre_rows = {}
         z_rows = {}
         total_feat = {}
         neg_mean = {}
         inv_std = {}
+        shift = {}
 
-        def product(block, step):
+        def prepare(unit):
+            block, r4 = divmod(unit, STEPS)
             grp, l = divmod(block, BRANCHES)
-            if step == 0:
-                y_feat[block] = blocks.tile([P, FEATURE_TILES, BANK], F32, name="y_feat")
-            for ft in (2 * step, 2 * step + 1):
-                lin = lin_psum.tile([P, BANK], F32, name="lin")
+            rt = GROUP_TILES * grp + r4
+            if l == 0:
+                quantise_row_tile(rt)
+            h_plus_b[unit] = units.tile([P, H], F32, name="h_plus_b")
+            nc.gpsimd.tensor_tensor(out=h_plus_b[unit][:], in0=h_sb[:, rt, :], in1=b_all[:, l, :], op=ALU.add)
+
+        def product(unit):
+            block, r4 = divmod(unit, STEPS)
+            grp, l = divmod(block, BRANCHES)
+            rt = GROUP_TILES * grp + r4
+            lin = lin_psum.tile([P, HALVES, BANK], F32, name="lin")
+            for half in range(HALVES):
                 for c in range(PASSES):
                     chunk = l * PASSES + c
                     nc.tensor.matmul_mx(
-                        out=lin[:],
-                        lhsT=w_words[:, chunk, 2 * P * ft : 2 * P * (ft + 1)].bitcast(FP4X4),
-                        lhsT_scale=w_scales[:, chunk, P * ft : P * (ft + 1)],
-                        rhs=h_codes[:, grp, c, :].bitcast(FP8X4),
-                        rhs_scale=h_scales[:, grp, c, :],
+                        out=lin[:, half, :],
+                        lhsT=h_codes[:, rt, c * P : (c + 1) * P].bitcast(FP8X4),
+                        lhsT_scale=h_scales[:, rt, c * P : (c + 1) * P],
+                        rhs=w_words[:, chunk, 2 * BANK * half : 2 * BANK * (half + 1)].bitcast(FP4X4),
+                        rhs_scale=w_scales[:, chunk, BANK * half : BANK * (half + 1)],
                         start=(c == 0),
                         stop=(c == PASSES - 1),
                     )
-                nc.scalar.activation(
-                    out=y_feat[block][:, ft, :], in_=lin[:], func=ACT.Identity, bias=column(0, l, ft), scale=1.0
-                )
-
-        def to_rows(block, r4):
-            grp, l = divmod(block, BRANCHES)
-            unit = (block, r4)
-            if r4 == 0:
-                pre_rows[block] = blocks.tile([P, GROUP_TILES, H], F32, name="pre_rows")
+            pre_rows[unit] = units.tile([P, H], F32, name="pre_rows")
             row_sums = stats.tile([P, HALVES], F32, name="row_sums")
             for half in range(HALVES):
-                y_rows = rows_psum.tile([P, BANK], F32, name="y_rows")
-                for q in range(BANK // P):
-                    nc.tensor.transpose(
-                        y_rows[:, P * q : P * (q + 1)],
-                        y_feat[block][:, (BANK // P) * half + q, P * r4 : P * (r4 + 1)],
-                        identity[:],
-                    )
                 cols = slice(BANK * half, BANK * (half + 1))
                 nc.vector.scalar_tensor_tensor(
-                    out=pre_rows[block][:, r4, cols],
-                    in0=y_rows[:],
+                    out=pre_rows[unit][:, cols],
+                    in0=lin[:, half, :],
                     scalar=1.0,
-                    in1=h_sb[:, GROUP_TILES * grp + r4, cols],
+                    in1=h_plus_b[unit][:, cols],
                     op0=ALU.mult,
                     op1=ALU.add,
                     accum_out=row_sums[:, half : half + 1],
@@ -187,7 +164,7 @@ def tile_advancedliquidneuralnetwork_pa_e_kernel(
             sum_squares = stats.tile([P, 1], F32, name="sum_squares")
             nc.scalar.activation(
                 out=squares[:],
-                in_=pre_rows[block][:, r4, :],
+                in_=pre_rows[unit][:],
                 func=ACT.Square,
                 bias=neg_mean[unit][:],
                 scale=1.0,
@@ -197,43 +174,62 @@ def tile_advancedliquidneuralnetwork_pa_e_kernel(
             nc.scalar.activation(
                 out=inv_std[unit][:], in_=sum_squares[:], func=ACT.Abs_reciprocal_sqrt, bias=eps[:], scale=1.0 / H
             )
+            shift[unit] = stats.tile([P, 1], F32, name="shift")
+            nc.scalar.activation(
+                out=shift[unit][:], in_=neg_mean[unit][:], func=ACT.Identity, scale=inv_std[unit][:]
+            )
 
-        def normalise(block, r4):
-            unit = (block, r4)
+        def normalise(unit):
+            block, r4 = divmod(unit, STEPS)
             if r4 == 0:
                 z_rows[block] = blocks.tile([P, GROUP_TILES, H], F32, name="z_rows")
-            nc.vector.tensor_scalar(
+            nc.scalar.activation(
                 out=z_rows[block][:, r4, :],
-                in0=pre_rows[block][:, r4, :],
-                scalar1=neg_mean[unit][:],
-                scalar2=inv_std[unit][:],
-                op0=ALU.add,
-                op1=ALU.mult,
+                in_=pre_rows[unit][:],
+                func=ACT.Identity,
+                bias=shift[unit][:],
+                scale=inv_std[unit][:],
             )
+
+        vector_columns = keep.tile([P, P], F32)
+        beta_sum = keep.tile([P, FEATURE_TILES], F32)
+
+        def vectors_to_columns():
+            vector_rows_f32 = keep.tile([P, P], F32, name="vector_rows_f32")
+            nc.vector.tensor_copy(out=vector_rows_f32[:], in_=vector_rows[:])
+            vector_bank = back_psum.tile([P, P], F32, tag="z_feat", name="vector_bank")
+            nc.tensor.transpose(vector_bank[:], vector_rows_f32[:], identity[:])
+            nc.vector.tensor_copy(out=vector_columns[:], in_=vector_bank[:])
+            nc.vector.tensor_tensor(
+                out=beta_sum[:], in0=vector_columns[:, 32:40], in1=vector_columns[:, 40:48], op=ALU.add
+            )
+            nc.vector.tensor_tensor(out=beta_sum[:], in0=beta_sum[:], in1=vector_columns[:, 48:56], op=ALU.add)
 
         def gain_and_add(block, step):
             grp, l = divmod(block, BRANCHES)
             if l == 0 and step == 0:
                 total_feat[grp] = blocks.tile([P, FEATURE_TILES, BANK], F32, name="total_feat")
             for ft in (2 * step, 2 * step + 1):
+                gain = vector_columns[:, FEATURE_TILES * l + ft : FEATURE_TILES * l + ft + 1]
                 z_feat = back_psum.tile([P, BANK], F32, name="z_feat")
                 for r4 in range(GROUP_TILES):
                     nc.tensor.transpose(
                         z_feat[:, P * r4 : P * (r4 + 1)], z_rows[block][:, r4, P * ft : P * (ft + 1)], identity[:]
                     )
                 if l == 0:
-                    nc.scalar.activation(
+                    nc.vector.tensor_scalar(
                         out=total_feat[grp][:, ft, :],
-                        in_=z_feat[:],
-                        func=ACT.Identity,
-                        bias=beta_sum[:, ft : ft + 1],
-                        scale=column(1, l, ft),
+                        in0=z_feat[:],
+                        scalar1=gain,
+                        scalar2=beta_sum[:, ft : ft + 1],
+                        op0=ALU.mult,
+                        op1=ALU.add,
                     )
                 else:
                     nc.vector.scalar_tensor_tensor(
                         out=total_feat[grp][:, ft, :],
                         in0=z_feat[:],
-                        scalar=column(1, l, ft),
+                        scalar=gain,
                         in1=total_feat[grp][:, ft, :],
                         op0=ALU.mult,
                         op1=ALU.add,
@@ -257,21 +253,21 @@ def tile_advancedliquidneuralnetwork_pa_e_kernel(
             rt = GROUP_TILES * grp + r4
             nc.sync.dma_start(out=out[rt * P : (rt + 1) * P, :], in_=result[:])
 
-        rows_at = LAG_ROWS
-        normalise_at = rows_at + LAG_NORMALISE
+        product_at = LAG_PRODUCT
+        normalise_at = product_at + LAG_NORMALISE
         back_at = normalise_at + LAG_BACK
         all_steps = BLOCKS * STEPS
         for now in range(all_steps + back_at + STEPS):
             if now < all_steps:
-                product(*divmod(now, STEPS))
-            if now == STEPS:
-                quantise_group(1)
-            if 0 <= now - rows_at < all_steps:
-                to_rows(*divmod(now - rows_at, STEPS))
+                prepare(now)
+            if now == LAG_PRODUCT:
+                vectors_to_columns()
+            if 0 <= now - normalise_at < all_steps:
+                normalise(now - normalise_at)
+            if 0 <= now - product_at < all_steps:
+                product(now - product_at)
             if 0 <= now - back_at < all_steps:
                 gain_and_add(*divmod(now - back_at, STEPS))
-            if 0 <= now - normalise_at < all_steps:
-                normalise(*divmod(now - normalise_at, STEPS))
             block, r4 = divmod(now - back_at, STEPS)
             if block > 0 and block % BRANCHES == 0:
                 finish(block // BRANCHES - 1, r4)

@@ -32,6 +32,7 @@ ROW_TILES = GROUPS * GROUP_TILES
 FLOPS = 2 * BRANCHES * ROWS * H * H
 
 LAG_PRODUCT = 2
+LAG_STATISTICS = 1
 LAG_NORMALISE = 1
 LAG_BACK = STEPS
 
@@ -45,7 +46,7 @@ def tile_advancedliquidneuralnetwork_pa_e_kernel(
         blocks = ctx.enter_context(tc.tile_pool(name="blocks", bufs=2))
         units = ctx.enter_context(tc.tile_pool(name="units", bufs=4))
         stats = ctx.enter_context(tc.tile_pool(name="stats", bufs=8))
-        lin_psum = ctx.enter_context(tc.psum_pool(name="lin_psum", bufs=2))
+        lin_psum = ctx.enter_context(tc.psum_pool(name="lin_psum", bufs=4))
         back_psum = ctx.enter_context(tc.psum_pool(name="back_psum", bufs=2))
         out_psum = ctx.enter_context(tc.psum_pool(name="out_psum", bufs=2))
         ctx.enter_context(tc.manual_schedule())
@@ -108,9 +109,12 @@ def tile_advancedliquidneuralnetwork_pa_e_kernel(
         pre_rows = {}
         z_rows = {}
         total_feat = {}
+        row_sums = {}
         neg_mean = {}
+        sum_squares = {}
         inv_std = {}
         shift = {}
+        result = {}
 
         def prepare(unit):
             block, r4 = divmod(unit, STEPS)
@@ -121,58 +125,67 @@ def tile_advancedliquidneuralnetwork_pa_e_kernel(
             h_plus_b[unit] = units.tile([P, H], F32, name="h_plus_b")
             nc.gpsimd.tensor_tensor(out=h_plus_b[unit][:], in0=h_sb[:, rt, :], in1=b_all[:, l, :], op=ALU.add)
 
-        def product(unit):
+        def product(unit, half):
             block, r4 = divmod(unit, STEPS)
             grp, l = divmod(block, BRANCHES)
             rt = GROUP_TILES * grp + r4
-            lin = lin_psum.tile([P, HALVES, BANK], F32, name="lin")
-            for half in range(HALVES):
-                for c in range(PASSES):
-                    chunk = l * PASSES + c
-                    nc.tensor.matmul_mx(
-                        out=lin[:, half, :],
-                        lhsT=h_codes[:, rt, c * P : (c + 1) * P].bitcast(FP8X4),
-                        lhsT_scale=h_scales[:, rt, c * P : (c + 1) * P],
-                        rhs=w_words[:, chunk, 2 * BANK * half : 2 * BANK * (half + 1)].bitcast(FP4X4),
-                        rhs_scale=w_scales[:, chunk, BANK * half : BANK * (half + 1)],
-                        start=(c == 0),
-                        stop=(c == PASSES - 1),
-                    )
-            pre_rows[unit] = units.tile([P, H], F32, name="pre_rows")
-            row_sums = stats.tile([P, HALVES], F32, name="row_sums")
-            for half in range(HALVES):
-                cols = slice(BANK * half, BANK * (half + 1))
-                nc.vector.scalar_tensor_tensor(
-                    out=pre_rows[unit][:, cols],
-                    in0=lin[:, half, :],
-                    scalar=1.0,
-                    in1=h_plus_b[unit][:, cols],
-                    op0=ALU.mult,
-                    op1=ALU.add,
-                    accum_out=row_sums[:, half : half + 1],
+            if half == 0:
+                pre_rows[unit] = units.tile([P, H], F32, name="pre_rows")
+                row_sums[unit] = stats.tile([P, HALVES], F32, name="row_sums")
+            lin = lin_psum.tile([P, BANK], F32, name="lin")
+            for c in range(PASSES):
+                chunk = l * PASSES + c
+                nc.tensor.matmul_mx(
+                    out=lin[:],
+                    lhsT=h_codes[:, rt, c * P : (c + 1) * P].bitcast(FP8X4),
+                    lhsT_scale=h_scales[:, rt, c * P : (c + 1) * P],
+                    rhs=w_words[:, chunk, 2 * BANK * half : 2 * BANK * (half + 1)].bitcast(FP4X4),
+                    rhs_scale=w_scales[:, chunk, BANK * half : BANK * (half + 1)],
+                    start=(c == 0),
+                    stop=(c == PASSES - 1),
                 )
+            cols = slice(BANK * half, BANK * (half + 1))
+            nc.vector.scalar_tensor_tensor(
+                out=pre_rows[unit][:, cols],
+                in0=lin[:],
+                scalar=1.0,
+                in1=h_plus_b[unit][:, cols],
+                op0=ALU.mult,
+                op1=ALU.add,
+                accum_out=row_sums[unit][:, half : half + 1],
+            )
+
+        def mean(unit):
             neg_mean[unit] = stats.tile([P, 1], F32, name="neg_mean")
             nc.vector.tensor_scalar(
                 out=neg_mean[unit][:],
-                in0=row_sums[:, 0:1],
-                scalar1=row_sums[:, 1:2],
+                in0=row_sums[unit][:, 0:1],
+                scalar1=row_sums[unit][:, 1:2],
                 scalar2=-1.0 / H,
                 op0=ALU.add,
                 op1=ALU.mult,
             )
+
+        def square(unit):
             squares = blocks.tile([P, H], BF16, name="squares")
-            sum_squares = stats.tile([P, 1], F32, name="sum_squares")
+            sum_squares[unit] = stats.tile([P, 1], F32, name="sum_squares")
             nc.scalar.activation(
                 out=squares[:],
                 in_=pre_rows[unit][:],
                 func=ACT.Square,
                 bias=neg_mean[unit][:],
                 scale=1.0,
-                accum_out=sum_squares[:],
+                accum_out=sum_squares[unit][:],
             )
+
+        def scale_and_shift(unit):
             inv_std[unit] = stats.tile([P, 1], F32, name="inv_std")
             nc.scalar.activation(
-                out=inv_std[unit][:], in_=sum_squares[:], func=ACT.Abs_reciprocal_sqrt, bias=eps[:], scale=1.0 / H
+                out=inv_std[unit][:],
+                in_=sum_squares[unit][:],
+                func=ACT.Abs_reciprocal_sqrt,
+                bias=eps[:],
+                scale=1.0 / H,
             )
             shift[unit] = stats.tile([P, 1], F32, name="shift")
             nc.scalar.activation(
@@ -205,56 +218,56 @@ def tile_advancedliquidneuralnetwork_pa_e_kernel(
             )
             nc.vector.tensor_tensor(out=beta_sum[:], in0=beta_sum[:], in1=vector_columns[:, 48:56], op=ALU.add)
 
-        def gain_and_add(block, step):
+        def gain_and_add(block, ft):
             grp, l = divmod(block, BRANCHES)
-            if l == 0 and step == 0:
+            if l == 0 and ft == 0:
                 total_feat[grp] = blocks.tile([P, FEATURE_TILES, BANK], F32, name="total_feat")
-            for ft in (2 * step, 2 * step + 1):
-                gain = vector_columns[:, FEATURE_TILES * l + ft : FEATURE_TILES * l + ft + 1]
-                z_feat = back_psum.tile([P, BANK], F32, name="z_feat")
-                for r4 in range(GROUP_TILES):
-                    nc.tensor.transpose(
-                        z_feat[:, P * r4 : P * (r4 + 1)], z_rows[block][:, r4, P * ft : P * (ft + 1)], identity[:]
-                    )
-                if l == 0:
-                    nc.vector.tensor_scalar(
-                        out=total_feat[grp][:, ft, :],
-                        in0=z_feat[:],
-                        scalar1=gain,
-                        scalar2=beta_sum[:, ft : ft + 1],
-                        op0=ALU.mult,
-                        op1=ALU.add,
-                    )
-                else:
-                    nc.vector.scalar_tensor_tensor(
-                        out=total_feat[grp][:, ft, :],
-                        in0=z_feat[:],
-                        scalar=gain,
-                        in1=total_feat[grp][:, ft, :],
-                        op0=ALU.mult,
-                        op1=ALU.add,
-                    )
+            gain = vector_columns[:, FEATURE_TILES * l + ft : FEATURE_TILES * l + ft + 1]
+            z_feat = back_psum.tile([P, BANK], F32, name="z_feat")
+            for r4 in range(GROUP_TILES):
+                nc.tensor.transpose(
+                    z_feat[:, P * r4 : P * (r4 + 1)], z_rows[block][:, r4, P * ft : P * (ft + 1)], identity[:]
+                )
+            if l == 0:
+                nc.vector.tensor_scalar(
+                    out=total_feat[grp][:, ft, :],
+                    in0=z_feat[:],
+                    scalar1=gain,
+                    scalar2=beta_sum[:, ft : ft + 1],
+                    op0=ALU.mult,
+                    op1=ALU.add,
+                )
+            else:
+                nc.vector.scalar_tensor_tensor(
+                    out=total_feat[grp][:, ft, :],
+                    in0=z_feat[:],
+                    scalar=gain,
+                    in1=total_feat[grp][:, ft, :],
+                    op0=ALU.mult,
+                    op1=ALU.add,
+                )
 
-        def finish(grp, r4):
-            result = blocks.tile([P, H], F32, name="result")
-            for half in range(HALVES):
-                out_rows = out_psum.tile([P, BANK], F32, name="out_rows")
-                for q in range(BANK // P):
-                    nc.tensor.transpose(
-                        out_rows[:, P * q : P * (q + 1)],
-                        total_feat[grp][:, (BANK // P) * half + q, P * r4 : P * (r4 + 1)],
-                        identity[:],
-                    )
-                cols = slice(BANK * half, BANK * (half + 1))
-                if half == 0:
-                    nc.scalar.copy(out=result[:, cols], in_=out_rows[:])
-                else:
-                    nc.vector.tensor_copy(out=result[:, cols], in_=out_rows[:])
-            rt = GROUP_TILES * grp + r4
-            nc.sync.dma_start(out=out[rt * P : (rt + 1) * P, :], in_=result[:])
+        def finish(grp, r4, half):
+            if half == 0:
+                result[grp] = blocks.tile([P, H], F32, name="result")
+            out_rows = out_psum.tile([P, BANK], F32, name="out_rows")
+            for q in range(BANK // P):
+                nc.tensor.transpose(
+                    out_rows[:, P * q : P * (q + 1)],
+                    total_feat[grp][:, (BANK // P) * half + q, P * r4 : P * (r4 + 1)],
+                    identity[:],
+                )
+            cols = slice(BANK * half, BANK * (half + 1))
+            if half == 0:
+                nc.scalar.copy(out=result[grp][:, cols], in_=out_rows[:])
+            else:
+                nc.vector.tensor_copy(out=result[grp][:, cols], in_=out_rows[:])
+                rt = GROUP_TILES * grp + r4
+                nc.sync.dma_start(out=out[rt * P : (rt + 1) * P, :], in_=result[grp][:])
 
         product_at = LAG_PRODUCT
-        normalise_at = product_at + LAG_NORMALISE
+        statistics_at = product_at + LAG_STATISTICS
+        normalise_at = statistics_at + LAG_NORMALISE
         back_at = normalise_at + LAG_BACK
         all_steps = BLOCKS * STEPS
         for now in range(all_steps + back_at + STEPS):
@@ -262,12 +275,19 @@ def tile_advancedliquidneuralnetwork_pa_e_kernel(
                 prepare(now)
             if now == LAG_PRODUCT:
                 vectors_to_columns()
+            if 0 <= now - statistics_at < all_steps:
+                square(now - statistics_at)
             if 0 <= now - normalise_at < all_steps:
                 normalise(now - normalise_at)
+            if 0 <= now - statistics_at < all_steps:
+                scale_and_shift(now - statistics_at)
+            for half in range(HALVES):
+                if 0 <= now - product_at < all_steps:
+                    product(now - product_at, half)
+                block, step = divmod(now - back_at, STEPS)
+                if 0 <= block < BLOCKS:
+                    gain_and_add(block, HALVES * step + half)
+                if block > 0 and block % BRANCHES == 0:
+                    finish(block // BRANCHES - 1, step, half)
             if 0 <= now - product_at < all_steps:
-                product(now - product_at)
-            if 0 <= now - back_at < all_steps:
-                gain_and_add(*divmod(now - back_at, STEPS))
-            block, r4 = divmod(now - back_at, STEPS)
-            if block > 0 and block % BRANCHES == 0:
-                finish(block // BRANCHES - 1, r4)
+                mean(now - product_at)

@@ -123,7 +123,7 @@ def tile_advancedliquidneuralnetwork_pa_e_kernel(
             if l == 0:
                 quantise_row_tile(rt)
             h_plus_b[unit] = units.tile([P, H], F32, name="h_plus_b")
-            nc.gpsimd.tensor_tensor(out=h_plus_b[unit][:], in0=h_sb[:, rt, :], in1=b_all[:, l, :], op=ALU.add)
+            nc.vector.tensor_tensor(out=h_plus_b[unit][:], in0=h_sb[:, rt, :], in1=b_all[:, l, :], op=ALU.add)
 
         def product(unit, half):
             block, r4 = divmod(unit, STEPS)
@@ -229,13 +229,12 @@ def tile_advancedliquidneuralnetwork_pa_e_kernel(
                     z_feat[:, P * r4 : P * (r4 + 1)], z_rows[block][:, r4, P * ft : P * (ft + 1)], identity[:]
                 )
             if l == 0:
-                nc.vector.tensor_scalar(
+                nc.scalar.activation(
                     out=total_feat[grp][:, ft, :],
-                    in0=z_feat[:],
-                    scalar1=gain,
-                    scalar2=beta_sum[:, ft : ft + 1],
-                    op0=ALU.mult,
-                    op1=ALU.add,
+                    in_=z_feat[:],
+                    func=ACT.Identity,
+                    bias=beta_sum[:, ft : ft + 1],
+                    scale=gain,
                 )
             else:
                 nc.vector.scalar_tensor_tensor(
@@ -257,11 +256,8 @@ def tile_advancedliquidneuralnetwork_pa_e_kernel(
                     total_feat[grp][:, (BANK // P) * half + q, P * r4 : P * (r4 + 1)],
                     identity[:],
                 )
-            cols = slice(BANK * half, BANK * (half + 1))
-            if half == 0:
-                nc.scalar.copy(out=result[grp][:, cols], in_=out_rows[:])
-            else:
-                nc.vector.tensor_copy(out=result[grp][:, cols], in_=out_rows[:])
+            nc.scalar.copy(out=result[grp][:, BANK * half : BANK * (half + 1)], in_=out_rows[:])
+            if half == HALVES - 1:
                 rt = GROUP_TILES * grp + r4
                 nc.sync.dma_start(out=out[rt * P : (rt + 1) * P, :], in_=result[grp][:])
 

@@ -49,7 +49,6 @@ def tile_advancedliquidneuralnetwork_pa_e_kernel(
         lin_psum = ctx.enter_context(tc.psum_pool(name="lin_psum", bufs=4))
         back_psum = ctx.enter_context(tc.psum_pool(name="back_psum", bufs=2))
         out_psum = ctx.enter_context(tc.psum_pool(name="out_psum", bufs=2))
-        ctx.enter_context(tc.manual_schedule())
 
         h_sb = keep.tile([P, ROW_TILES, H], BF16)
         w_words = keep.tile([P, BRANCHES * PASSES, 2 * H], U8, align_bytes=64)
@@ -123,7 +122,7 @@ def tile_advancedliquidneuralnetwork_pa_e_kernel(
             if l == 0:
                 quantise_row_tile(rt)
             h_plus_b[unit] = units.tile([P, H], F32, name="h_plus_b")
-            nc.vector.tensor_tensor(out=h_plus_b[unit][:], in0=h_sb[:, rt, :], in1=b_all[:, l, :], op=ALU.add)
+            nc.gpsimd.tensor_tensor(out=h_plus_b[unit][:], in0=h_sb[:, rt, :], in1=b_all[:, l, :], op=ALU.add)
 
         def product(unit, half):
             block, r4 = divmod(unit, STEPS)
@@ -229,12 +228,13 @@ def tile_advancedliquidneuralnetwork_pa_e_kernel(
                     z_feat[:, P * r4 : P * (r4 + 1)], z_rows[block][:, r4, P * ft : P * (ft + 1)], identity[:]
                 )
             if l == 0:
-                nc.scalar.activation(
+                nc.vector.tensor_scalar(
                     out=total_feat[grp][:, ft, :],
-                    in_=z_feat[:],
-                    func=ACT.Identity,
-                    bias=beta_sum[:, ft : ft + 1],
-                    scale=gain,
+                    in0=z_feat[:],
+                    scalar1=gain,
+                    scalar2=beta_sum[:, ft : ft + 1],
+                    op0=ALU.mult,
+                    op1=ALU.add,
                 )
             else:
                 nc.vector.scalar_tensor_tensor(
@@ -256,8 +256,11 @@ def tile_advancedliquidneuralnetwork_pa_e_kernel(
                     total_feat[grp][:, (BANK // P) * half + q, P * r4 : P * (r4 + 1)],
                     identity[:],
                 )
-            nc.scalar.copy(out=result[grp][:, BANK * half : BANK * (half + 1)], in_=out_rows[:])
-            if half == HALVES - 1:
+            cols = slice(BANK * half, BANK * (half + 1))
+            if half == 0:
+                nc.scalar.copy(out=result[grp][:, cols], in_=out_rows[:])
+            else:
+                nc.vector.tensor_copy(out=result[grp][:, cols], in_=out_rows[:])
                 rt = GROUP_TILES * grp + r4
                 nc.sync.dma_start(out=out[rt * P : (rt + 1) * P, :], in_=result[grp][:])
 

@@ -34,7 +34,7 @@ FLOPS = 2 * BRANCHES * ROWS * H * H
 LAG_PRODUCT = 2
 LAG_STATISTICS = 1
 LAG_NORMALISE = 1
-LAG_BACK = STEPS
+LAG_BACK = STEPS + 1
 
 
 def tile_advancedliquidneuralnetwork_pa_e_kernel(
@@ -47,8 +47,7 @@ def tile_advancedliquidneuralnetwork_pa_e_kernel(
         units = ctx.enter_context(tc.tile_pool(name="units", bufs=4))
         stats = ctx.enter_context(tc.tile_pool(name="stats", bufs=8))
         lin_psum = ctx.enter_context(tc.psum_pool(name="lin_psum", bufs=4))
-        back_psum = ctx.enter_context(tc.psum_pool(name="back_psum", bufs=2))
-        out_psum = ctx.enter_context(tc.psum_pool(name="out_psum", bufs=2))
+        turn_psum = ctx.enter_context(tc.psum_pool(name="turn_psum", bufs=4))
 
         h_sb = keep.tile([P, ROW_TILES, H], BF16)
         w_words = keep.tile([P, BRANCHES * PASSES, 2 * H], U8, align_bytes=64)
@@ -90,7 +89,7 @@ def tile_advancedliquidneuralnetwork_pa_e_kernel(
 
         def quantise_row_tile(rt):
             pairs = h_sb[:, rt, :].bitcast(F32)
-            turned = out_psum.tile([P, PASSES, 2, P], F32, tag="out_rows", name="turned")
+            turned = turn_psum.tile([P, PASSES, 2, P], F32, tag="turn", name="turned")
             for c in range(PASSES):
                 for u in range(2):
                     nc.tensor.transpose(
@@ -209,7 +208,7 @@ def tile_advancedliquidneuralnetwork_pa_e_kernel(
         def vectors_to_columns():
             vector_rows_f32 = keep.tile([P, P], F32, name="vector_rows_f32")
             nc.vector.tensor_copy(out=vector_rows_f32[:], in_=vector_rows[:])
-            vector_bank = back_psum.tile([P, P], F32, tag="z_feat", name="vector_bank")
+            vector_bank = turn_psum.tile([P, P], F32, tag="turn", name="vector_bank")
             nc.tensor.transpose(vector_bank[:], vector_rows_f32[:], identity[:])
             nc.vector.tensor_copy(out=vector_columns[:], in_=vector_bank[:])
             nc.vector.tensor_tensor(
@@ -222,7 +221,7 @@ def tile_advancedliquidneuralnetwork_pa_e_kernel(
             if l == 0 and ft == 0:
                 total_feat[grp] = blocks.tile([P, FEATURE_TILES, BANK], F32, name="total_feat")
             gain = vector_columns[:, FEATURE_TILES * l + ft : FEATURE_TILES * l + ft + 1]
-            z_feat = back_psum.tile([P, BANK], F32, name="z_feat")
+            z_feat = turn_psum.tile([P, BANK], F32, tag="turn", name="z_feat")
             for r4 in range(GROUP_TILES):
                 nc.tensor.transpose(
                     z_feat[:, P * r4 : P * (r4 + 1)], z_rows[block][:, r4, P * ft : P * (ft + 1)], identity[:]
@@ -249,7 +248,7 @@ def tile_advancedliquidneuralnetwork_pa_e_kernel(
         def finish(grp, r4, half):
             if half == 0:
                 result[grp] = blocks.tile([P, H], F32, name="result")
-            out_rows = out_psum.tile([P, BANK], F32, name="out_rows")
+            out_rows = turn_psum.tile([P, BANK], F32, tag="turn", name="out_rows")
             for q in range(BANK // P):
                 nc.tensor.transpose(
                     out_rows[:, P * q : P * (q + 1)],
@@ -280,13 +279,15 @@ def tile_advancedliquidneuralnetwork_pa_e_kernel(
                 normalise(now - normalise_at)
             if 0 <= now - statistics_at < all_steps:
                 scale_and_shift(now - statistics_at)
-            for half in range(HALVES):
-                if 0 <= now - product_at < all_steps:
+            if 0 <= now - product_at < all_steps:
+                for half in range(HALVES):
                     product(now - product_at, half)
-                block, step = divmod(now - back_at, STEPS)
-                if 0 <= block < BLOCKS:
+            block, step = divmod(now - back_at, STEPS)
+            if 0 <= block < BLOCKS:
+                for half in range(HALVES):
                     gain_and_add(block, HALVES * step + half)
-                if block > 0 and block % BRANCHES == 0:
+            if block > 0 and block % BRANCHES == 0:
+                for half in range(HALVES):
                     finish(block // BRANCHES - 1, step, half)
             if 0 <= now - product_at < all_steps:
                 mean(now - product_at)

@@ -56,6 +56,13 @@ def tile_advancedliquidneuralnetwork_pa_e_kernel(
         vector_rows = keep.tile([P, P], BF16)
         nc.vector.memset(vector_rows[:], 0.0)
         b_all = keep.tile([P, BRANCHES, H], BF16)
+        b_rows = keep.tile([P, H], BF16)
+        nc.gpsimd.memset(b_rows[:], 0.0)
+        pick = keep.tile([P, BRANCHES, P], BF16)
+        nc.gpsimd.memset(pick[:], 0.0)
+        for l in range(BRANCHES):
+            nc.gpsimd.memset(pick[32 * l : 32 * l + 1, l, :], 1.0)
+            nc.scalar.dma_start(out=b_rows[32 * l : 32 * l + 1, :], in_=b_liq[l : l + 1, :])
 
         nc.sync.dma_start(out=h_sb[:, 0, :], in_=h[0:P, :])
         for quad in range(4):
@@ -76,13 +83,21 @@ def tile_advancedliquidneuralnetwork_pa_e_kernel(
                 out=vector_rows[32 * kind : 32 * kind + BRANCHES * FEATURE_TILES, :],
                 in_=vectors.rearrange("l (ft p) -> (l ft) p", p=P),
             )
-        for l in range(BRANCHES):
-            nc.scalar.dma_start(out=b_all[:, l, :], in_=b_liq[l].partition_broadcast(P))
 
         identity = keep.tile([P, P], F32)
         make_identity(nc, identity[:])
         eps = keep.tile([P, 1], F32)
         nc.vector.memset(eps[:], LN_EPS)
+
+        def spread_bias(l):
+            for half in range(HALVES):
+                cols = slice(BANK * half, BANK * (half + 1))
+                b_bank = turn_psum.tile([P, BANK], F32, tag="turn", name="b_bank")
+                nc.tensor.matmul(out=b_bank[:], lhsT=pick[:, l, :], rhs=b_rows[:, cols], start=True, stop=True)
+                if l == 0:
+                    nc.vector.tensor_copy(out=b_all[:, l, cols], in_=b_bank[:])
+                else:
+                    nc.scalar.copy(out=b_all[:, l, cols], in_=b_bank[:])
 
         h_codes = keep.tile([P, ROW_TILES, PASSES * P], U32, align_bytes=64)
         h_scales = keep.tile([P, ROW_TILES, PASSES * P], U8, align_bytes=64)
@@ -269,6 +284,8 @@ def tile_advancedliquidneuralnetwork_pa_e_kernel(
         back_at = normalise_at + LAG_BACK
         all_steps = BLOCKS * STEPS
         for now in range(all_steps + back_at + STEPS):
+            if now < BRANCHES:
+                spread_bias(now)
             if now < all_steps:
                 prepare(now)
             if now == LAG_PRODUCT:

@@ -46,8 +46,9 @@ def tile_advancedliquidneuralnetwork_pa_e_kernel(
         blocks = ctx.enter_context(tc.tile_pool(name="blocks", bufs=2))
         units = ctx.enter_context(tc.tile_pool(name="units", bufs=4))
         stats = ctx.enter_context(tc.tile_pool(name="stats", bufs=8))
-        lin_psum = ctx.enter_context(tc.psum_pool(name="lin_psum", bufs=4))
-        turn_psum = ctx.enter_context(tc.psum_pool(name="turn_psum", bufs=4))
+        lin_psum = ctx.enter_context(tc.psum_pool(name="lin_psum", bufs=3))
+        turn_psum = ctx.enter_context(tc.psum_pool(name="turn_psum", bufs=3))
+        gain_psum = ctx.enter_context(tc.psum_pool(name="gain_psum", bufs=1))
 
         h_sb = keep.tile([P, ROW_TILES, H], BF16)
         w_words = keep.tile([P, BRANCHES * PASSES, 2 * H], U8, align_bytes=64)
@@ -58,11 +59,13 @@ def tile_advancedliquidneuralnetwork_pa_e_kernel(
         b_all = keep.tile([P, BRANCHES, H], BF16)
         b_rows = keep.tile([P, H], BF16)
         nc.gpsimd.memset(b_rows[:], 0.0)
-        pick = keep.tile([P, BRANCHES, P], BF16)
+        pick = keep.tile([P, BRANCHES + 1, P], BF16)
         nc.gpsimd.memset(pick[:], 0.0)
         for l in range(BRANCHES):
             nc.gpsimd.memset(pick[32 * l : 32 * l + 1, l, :], 1.0)
             nc.scalar.dma_start(out=b_rows[32 * l : 32 * l + 1, :], in_=b_liq[l : l + 1, :])
+        nc.gpsimd.memset(pick[96:97, BRANCHES, :], 1.0)
+        nc.scalar.dma_start(out=b_rows[96:97, :], in_=g_liq[BRANCHES - 1 : BRANCHES, :])
 
         nc.sync.dma_start(out=h_sb[:, 0, :], in_=h[0:P, :])
         for quad in range(4):
@@ -99,6 +102,13 @@ def tile_advancedliquidneuralnetwork_pa_e_kernel(
                 else:
                     nc.scalar.copy(out=b_all[:, l, cols], in_=b_bank[:])
 
+        g_last = [gain_psum.tile([P, BANK], F32, name="g_last%d" % half) for half in range(HALVES)]
+
+        def spread_gain():
+            for half in range(HALVES):
+                cols = slice(BANK * half, BANK * (half + 1))
+                nc.tensor.matmul(out=g_last[half][:], lhsT=pick[:, BRANCHES, :], rhs=b_rows[:, cols], start=True, stop=True)
+
         h_codes = keep.tile([P, ROW_TILES, PASSES * P], U32, align_bytes=64)
         h_scales = keep.tile([P, ROW_TILES, PASSES * P], U8, align_bytes=64)
 
@@ -128,6 +138,7 @@ def tile_advancedliquidneuralnetwork_pa_e_kernel(
         inv_std = {}
         shift = {}
         result = {}
+        gained = {}
 
         def prepare(unit):
             block, r4 = divmod(unit, STEPS)
@@ -200,10 +211,50 @@ def tile_advancedliquidneuralnetwork_pa_e_kernel(
                 bias=eps[:],
                 scale=1.0 / H,
             )
+            if (unit // STEPS) % BRANCHES == BRANCHES - 1:
+                return
             shift[unit] = stats.tile([P, 1], F32, name="shift")
             nc.scalar.activation(
                 out=shift[unit][:], in_=neg_mean[unit][:], func=ACT.Identity, scale=inv_std[unit][:]
             )
+
+        def centre_and_gain(unit):
+            gained[unit] = units.tile([P, H], F32, name="gained")
+            for half in range(HALVES):
+                cols = slice(BANK * half, BANK * (half + 1))
+                nc.vector.scalar_tensor_tensor(
+                    out=gained[unit][:, cols],
+                    in0=pre_rows[unit][:, cols],
+                    scalar=neg_mean[unit][:],
+                    in1=g_last[half][:],
+                    op0=ALU.add,
+                    op1=ALU.mult,
+                )
+
+        def finish_rows(unit, half):
+            block, r4 = divmod(unit, STEPS)
+            grp = block // BRANCHES
+            if half == 0:
+                result[grp] = blocks.tile([P, H], F32, name="result")
+            out_rows = turn_psum.tile([P, BANK], F32, tag="turn", name="out_rows")
+            for q in range(BANK // P):
+                nc.tensor.transpose(
+                    out_rows[:, P * q : P * (q + 1)],
+                    total_feat[grp][:, (BANK // P) * half + q, P * r4 : P * (r4 + 1)],
+                    identity[:],
+                )
+            cols = slice(BANK * half, BANK * (half + 1))
+            nc.vector.scalar_tensor_tensor(
+                out=result[grp][:, cols],
+                in0=gained[unit][:, cols],
+                scalar=inv_std[unit][:],
+                in1=out_rows[:],
+                op0=ALU.mult,
+                op1=ALU.add,
+            )
+            if half == HALVES - 1:
+                rt = GROUP_TILES * grp + r4
+                nc.sync.dma_start(out=out[rt * P : (rt + 1) * P, :], in_=result[grp][:])
 
         def normalise(unit):
             block, r4 = divmod(unit, STEPS)
@@ -242,13 +293,12 @@ def tile_advancedliquidneuralnetwork_pa_e_kernel(
                     z_feat[:, P * r4 : P * (r4 + 1)], z_rows[block][:, r4, P * ft : P * (ft + 1)], identity[:]
                 )
             if l == 0:
-                nc.vector.tensor_scalar(
+                nc.scalar.activation(
                     out=total_feat[grp][:, ft, :],
-                    in0=z_feat[:],
-                    scalar1=gain,
-                    scalar2=beta_sum[:, ft : ft + 1],
-                    op0=ALU.mult,
-                    op1=ALU.add,
+                    in_=z_feat[:],
+                    func=ACT.Identity,
+                    bias=beta_sum[:, ft : ft + 1],
+                    scale=gain,
                 )
             else:
                 nc.vector.scalar_tensor_tensor(
@@ -290,9 +340,13 @@ def tile_advancedliquidneuralnetwork_pa_e_kernel(
                 prepare(now)
             if now == LAG_PRODUCT:
                 vectors_to_columns()
+            if now == BRANCHES:
+                spread_gain()
             if 0 <= now - statistics_at < all_steps:
                 square(now - statistics_at)
-            if 0 <= now - normalise_at < all_steps:
+                if ((now - statistics_at) // STEPS) % BRANCHES == BRANCHES - 1:
+                    centre_and_gain(now - statistics_at)
+            if 0 <= now - normalise_at < all_steps and ((now - normalise_at) // STEPS) % BRANCHES < BRANCHES - 1:
                 normalise(now - normalise_at)
             if 0 <= now - statistics_at < all_steps:
                 scale_and_shift(now - statistics_at)
@@ -300,11 +354,11 @@ def tile_advancedliquidneuralnetwork_pa_e_kernel(
                 for half in range(HALVES):
                     product(now - product_at, half)
             block, step = divmod(now - back_at, STEPS)
-            if 0 <= block < BLOCKS:
+            if 0 <= block < BLOCKS and block % BRANCHES < BRANCHES - 1:
                 for half in range(HALVES):
                     gain_and_add(block, HALVES * step + half)
-            if block > 0 and block % BRANCHES == 0:
+            if 0 <= block < BLOCKS and block % BRANCHES == BRANCHES - 1:
                 for half in range(HALVES):
-                    finish(block // BRANCHES - 1, step, half)
+                    finish_rows(STEPS * block + step, half)
             if 0 <= now - product_at < all_steps:
                 mean(now - product_at)

@@ -58,7 +58,7 @@ def tile_advancedliquidneuralnetwork_pa_e_kernel(
         nc.vector.memset(vector_rows[:], 0.0)
         b_all = keep.tile([P, BRANCHES, H], BF16)
         b_rows = keep.tile([P, H], BF16)
-        nc.gpsimd.memset(b_rows[:], 0.0)
+        nc.gpsimd.memset(b_rows[:].bitcast(F32), 0.0)
         pick = keep.tile([P, BRANCHES + 1, P], BF16)
         nc.gpsimd.memset(pick[:], 0.0)
         for l in range(BRANCHES):
@@ -147,7 +147,11 @@ def tile_advancedliquidneuralnetwork_pa_e_kernel(
             if l == 0:
                 quantise_row_tile(rt)
             h_plus_b[unit] = units.tile([P, H], F32, name="h_plus_b")
-            nc.gpsimd.tensor_tensor(out=h_plus_b[unit][:], in0=h_sb[:, rt, :], in1=b_all[:, l, :], op=ALU.add)
+            for half in range(HALVES):
+                cols = slice(BANK * half, BANK * (half + 1))
+                nc.gpsimd.tensor_tensor(
+                    out=h_plus_b[unit][:, cols], in0=h_sb[:, rt, cols], in1=b_all[:, l, cols], op=ALU.add
+                )
 
         def product(unit, half):
             block, r4 = divmod(unit, STEPS)

@@ -53,7 +53,8 @@ def tile_advancedliquidneuralnetwork_pa_e_kernel(
         h_sb = keep.tile([P, ROW_TILES, H], BF16)
         w_words = keep.tile([P, BRANCHES * PASSES, 2 * H], U8, align_bytes=64)
         w_scales = keep.tile([P, BRANCHES * PASSES, H], U8, align_bytes=64)
-        nc.vector.memset(w_scales[:].bitcast(I32), 0)
+        for l in range(BRANCHES):
+            nc.vector.memset(w_scales[:, PASSES * l : PASSES * (l + 1), :].bitcast(I32), 0)
         vector_rows = keep.tile([P, P], BF16)
         nc.vector.memset(vector_rows[:], 0.0)
         b_all = keep.tile([P, BRANCHES, H], BF16)
@@ -67,18 +68,22 @@ def tile_advancedliquidneuralnetwork_pa_e_kernel(
         nc.gpsimd.memset(pick[96:97, BRANCHES, :], 1.0)
         nc.scalar.dma_start(out=b_rows[96:97, :], in_=g_liq[BRANCHES - 1 : BRANCHES, :])
 
+        def load_weights(l):
+            chunks = slice(PASSES * l, PASSES * (l + 1))
+            for quad in range(4):
+                nc.sync.dma_start(
+                    out=w_scales[32 * quad : 32 * quad + 4, chunks, :].bitcast(I32),
+                    in_=W_liq_scales[chunks, 4 * quad : 4 * quad + 4, :].rearrange("c r n -> r c n").bitcast(I32),
+                )
+            for chunk in range(PASSES * l, PASSES * (l + 1)):
+                nc.sync.dma_start(out=w_words[:, chunk, :].bitcast(I32), in_=W_liq_words[chunk].bitcast(I32))
+
         nc.sync.dma_start(out=h_sb[:, 0, :], in_=h[0:P, :])
-        for quad in range(4):
-            nc.sync.dma_start(
-                out=w_scales[32 * quad : 32 * quad + 4, :, :].bitcast(I32),
-                in_=W_liq_scales[:, 4 * quad : 4 * quad + 4, :].rearrange("c r n -> r c n").bitcast(I32),
-            )
-        for chunk in range(PASSES):
-            nc.sync.dma_start(out=w_words[:, chunk, :].bitcast(I32), in_=W_liq_words[chunk].bitcast(I32))
+        load_weights(0)
         for rt in range(1, GROUP_TILES):
             nc.sync.dma_start(out=h_sb[:, rt, :], in_=h[rt * P : (rt + 1) * P, :])
-        for chunk in range(PASSES, BRANCHES * PASSES):
-            nc.sync.dma_start(out=w_words[:, chunk, :].bitcast(I32), in_=W_liq_words[chunk].bitcast(I32))
+        for l in range(1, BRANCHES):
+            load_weights(l)
         for rt in range(GROUP_TILES, ROW_TILES):
             nc.sync.dma_start(out=h_sb[:, rt, :], in_=h[rt * P : (rt + 1) * P, :])
         for kind, vectors in enumerate((g_liq, beta_liq)):
@@ -121,7 +126,7 @@ def tile_advancedliquidneuralnetwork_pa_e_kernel(
                         turned[:, c, u, :], pairs[:, 256 * c + u : 256 * (c + 1) : 2], identity[:]
                     )
             grouped = blocks.tile([P, PASSES, P, 2], F32, align_bytes=64, name="grouped")
-            nc.vector.tensor_copy(out=grouped[:], in_=turned[:].rearrange("p c u r -> p c r u"))
+            nc.scalar.copy(out=grouped[:], in_=turned[:].rearrange("p c u r -> p c r u"))
             nc.vector.quantize_mx(
                 out=h_codes[:, rt, :].bitcast(FP8X4),
                 scales=h_scales[:, rt, :],
@@ -147,11 +152,7 @@ def tile_advancedliquidneuralnetwork_pa_e_kernel(
             if l == 0:
                 quantise_row_tile(rt)
             h_plus_b[unit] = units.tile([P, H], F32, name="h_plus_b")
-            for half in range(HALVES):
-                cols = slice(BANK * half, BANK * (half + 1))
-                nc.gpsimd.tensor_tensor(
-                    out=h_plus_b[unit][:, cols], in0=h_sb[:, rt, cols], in1=b_all[:, l, cols], op=ALU.add
-                )
+            nc.gpsimd.tensor_tensor(out=h_plus_b[unit][:], in0=h_sb[:, rt, :], in1=b_all[:, l, :], op=ALU.add)
 
         def product(unit, half):
             block, r4 = divmod(unit, STEPS)
@@ -215,7 +216,7 @@ def tile_advancedliquidneuralnetwork_pa_e_kernel(
                 bias=eps[:],
                 scale=1.0 / H,
             )
-            if (unit // STEPS) % BRANCHES == BRANCHES - 1:
+            if (unit // STEPS) % BRANCHES == BRANCHES - 1 or unit % STEPS == 0:
                 return
             shift[unit] = stats.tile([P, 1], F32, name="shift")
             nc.scalar.activation(
@@ -256,14 +257,23 @@ def tile_advancedliquidneuralnetwork_pa_e_kernel(
                 op0=ALU.mult,
                 op1=ALU.add,
             )
-            if half == HALVES - 1:
-                rt = GROUP_TILES * grp + r4
-                nc.sync.dma_start(out=out[rt * P : (rt + 1) * P, :], in_=result[grp][:])
+            rt = GROUP_TILES * grp + r4
+            nc.sync.dma_start(out=out[rt * P : (rt + 1) * P, cols], in_=result[grp][:, cols])
 
         def normalise(unit):
             block, r4 = divmod(unit, STEPS)
             if r4 == 0:
                 z_rows[block] = blocks.tile([P, GROUP_TILES, H], F32, name="z_rows")
+            if r4 == 0:
+                nc.gpsimd.tensor_scalar(
+                    out=z_rows[block][:, r4, :],
+                    in0=pre_rows[unit][:],
+                    scalar1=neg_mean[unit][:],
+                    scalar2=inv_std[unit][:],
+                    op0=ALU.add,
+                    op1=ALU.mult,
+                )
+                return
             nc.scalar.activation(
                 out=z_rows[block][:, r4, :],
                 in_=pre_rows[unit][:],

@@ -35,6 +35,7 @@ LAG_PRODUCT = 2
 LAG_STATISTICS = 1
 LAG_NORMALISE = 1
 LAG_BACK = STEPS + 1
+VECTOR_ADDS = (0, 2, 4, 6)
 
 
 def tile_advancedliquidneuralnetwork_pa_e_kernel(
@@ -107,12 +108,13 @@ def tile_advancedliquidneuralnetwork_pa_e_kernel(
                 else:
                     nc.scalar.copy(out=b_all[:, l, cols], in_=b_bank[:])
 
-        g_last = [gain_psum.tile([P, BANK], F32, name="g_last%d" % half) for half in range(HALVES)]
+        wide = {}
 
-        def spread_gain():
+        def spread_wide(row):
             for half in range(HALVES):
                 cols = slice(BANK * half, BANK * (half + 1))
-                nc.tensor.matmul(out=g_last[half][:], lhsT=pick[:, BRANCHES, :], rhs=b_rows[:, cols], start=True, stop=True)
+                wide[half] = gain_psum.tile([P, BANK], F32, tag="wide%d" % half, name="wide%d" % half)
+                nc.tensor.matmul(out=wide[half][:], lhsT=pick[:, row, :], rhs=b_rows[:, cols], start=True, stop=True)
 
         h_codes = keep.tile([P, ROW_TILES, PASSES * P], U32, align_bytes=64)
         h_scales = keep.tile([P, ROW_TILES, PASSES * P], U8, align_bytes=64)
@@ -152,6 +154,11 @@ def tile_advancedliquidneuralnetwork_pa_e_kernel(
             if l == 0:
                 quantise_row_tile(rt)
             h_plus_b[unit] = units.tile([P, H], F32, name="h_plus_b")
+            if unit in VECTOR_ADDS:
+                for half in range(HALVES):
+                    cols = slice(BANK * half, BANK * (half + 1))
+                    nc.vector.tensor_tensor(out=h_plus_b[unit][:, cols], in0=h_sb[:, rt, cols], in1=wide[half][:], op=ALU.add)
+                return
             nc.gpsimd.tensor_tensor(out=h_plus_b[unit][:], in0=h_sb[:, rt, :], in1=b_all[:, l, :], op=ALU.add)
 
         def product(unit, half):
@@ -231,7 +238,7 @@ def tile_advancedliquidneuralnetwork_pa_e_kernel(
                     out=gained[unit][:, cols],
                     in0=pre_rows[unit][:, cols],
                     scalar=neg_mean[unit][:],
-                    in1=g_last[half][:],
+                    in1=wide[half][:],
                     op0=ALU.add,
                     op1=ALU.mult,
                 )
@@ -350,12 +357,12 @@ def tile_advancedliquidneuralnetwork_pa_e_kernel(
         for now in range(all_steps + back_at + STEPS):
             if now < BRANCHES:
                 spread_bias(now)
+            if now % STEPS == 0 and now // STEPS < BRANCHES:
+                spread_wide((0, 1, BRANCHES)[now // STEPS])
             if now < all_steps:
                 prepare(now)
             if now == LAG_PRODUCT:
                 vectors_to_columns()
-            if now == BRANCHES:
-                spread_gain()
             if 0 <= now - statistics_at < all_steps:
                 square(now - statistics_at)
                 if ((now - statistics_at) // STEPS) % BRANCHES == BRANCHES - 1:

@@ -28,14 +28,39 @@ HALVES = H // BANK
 BLOCKS = GROUPS * BRANCHES
 STEPS = GROUP_TILES
 ROW_TILES = GROUPS * GROUP_TILES
+UNITS = BLOCKS * STEPS
+LAST = BRANCHES - 1
 
 FLOPS = 2 * BRANCHES * ROWS * H * H
 
-LAG_PRODUCT = 2
-LAG_STATISTICS = 1
-LAG_NORMALISE = 1
-LAG_BACK = STEPS + 1
-VECTOR_ADDS = (0, 2, 4, 6)
+LEAD = 3
+LAG_TURN = (4, 4)
+LAG_GROUP = (4, 4)
+LAG_QUANT = (3, 2)
+LAG_ADD_V = 4
+LAG_ADD_G = 3
+LAG_SQUARE = 2
+LAG_CENTRE = 0
+LAG_NORMALISE = 2
+LAG_GAIN = 3
+LAG_FINISH = 0
+VECTOR_ADDS = (0, 4, 5)
+GPSIMD_NORMALISES = (4, 5, 6, 16, 17)
+OWN_TILES = ((1, 4), (1, 5), (1, 6), (1, 7), (4, 4), (4, 5), (4, 6), (4, 7))
+VECTOR_FIRST = ((0, 0), (0, 1), (3, 0))
+GAINS_A_STEP = (2, 2, 0, 2, 4, 0)
+FINISHES_A_STEP = (1, 1)
+BUFS_ADD_G = 4
+BUFS_ADD_V = 2
+BUFS_PRE = 6
+BUFS_GAINED = 7
+BUFS_FEAT = 3
+PIN = True
+WARM = True
+ORDER = "pfstwacinmkgqrvb"
+SPREAD_AT = (0, 1, 3)
+COLUMNS_AT = 0
+LOADS = "h0 h1 w0 h2 h3 w1 w2 h4 h5 h6 h7"
 
 
 def tile_advancedliquidneuralnetwork_pa_e_kernel(
@@ -49,7 +74,7 @@ def tile_advancedliquidneuralnetwork_pa_e_kernel(
         stats = ctx.enter_context(tc.tile_pool(name="stats", bufs=8))
         lin_psum = ctx.enter_context(tc.psum_pool(name="lin_psum", bufs=3))
         turn_psum = ctx.enter_context(tc.psum_pool(name="turn_psum", bufs=3))
-        gain_psum = ctx.enter_context(tc.psum_pool(name="gain_psum", bufs=1))
+        wide_psum = ctx.enter_context(tc.psum_pool(name="wide_psum", bufs=1))
 
         h_sb = keep.tile([P, ROW_TILES, H], BF16)
         w_words = keep.tile([P, BRANCHES * PASSES, 2 * H], U8, align_bytes=64)
@@ -67,7 +92,12 @@ def tile_advancedliquidneuralnetwork_pa_e_kernel(
             nc.gpsimd.memset(pick[32 * l : 32 * l + 1, l, :], 1.0)
             nc.scalar.dma_start(out=b_rows[32 * l : 32 * l + 1, :], in_=b_liq[l : l + 1, :])
         nc.gpsimd.memset(pick[96:97, BRANCHES, :], 1.0)
-        nc.scalar.dma_start(out=b_rows[96:97, :], in_=g_liq[BRANCHES - 1 : BRANCHES, :])
+        nc.scalar.dma_start(out=b_rows[96:97, :], in_=g_liq[LAST : LAST + 1, :])
+        eps = keep.tile([P, 1], F32)
+        nc.vector.memset(eps[:], LN_EPS)
+        if WARM:
+            warm = keep.tile([P, 1], F32)
+            nc.scalar.activation(out=warm[:], in_=eps[:], func=ACT.Abs_reciprocal_sqrt, bias=eps[:], scale=1.0)
 
         def load_weights(l):
             chunks = slice(PASSES * l, PASSES * (l + 1))
@@ -79,14 +109,12 @@ def tile_advancedliquidneuralnetwork_pa_e_kernel(
             for chunk in range(PASSES * l, PASSES * (l + 1)):
                 nc.sync.dma_start(out=w_words[:, chunk, :].bitcast(I32), in_=W_liq_words[chunk].bitcast(I32))
 
-        nc.sync.dma_start(out=h_sb[:, 0, :], in_=h[0:P, :])
-        load_weights(0)
-        for rt in range(1, GROUP_TILES):
-            nc.sync.dma_start(out=h_sb[:, rt, :], in_=h[rt * P : (rt + 1) * P, :])
-        for l in range(1, BRANCHES):
-            load_weights(l)
-        for rt in range(GROUP_TILES, ROW_TILES):
-            nc.sync.dma_start(out=h_sb[:, rt, :], in_=h[rt * P : (rt + 1) * P, :])
+        for item in LOADS.split(" "):
+            number = int(item[1:])
+            if item[0] == "h":
+                nc.sync.dma_start(out=h_sb[:, number, :], in_=h[number * P : (number + 1) * P, :])
+            else:
+                load_weights(number)
         for kind, vectors in enumerate((g_liq, beta_liq)):
             nc.scalar.dma_start(
                 out=vector_rows[32 * kind : 32 * kind + BRANCHES * FEATURE_TILES, :],
@@ -95,50 +123,50 @@ def tile_advancedliquidneuralnetwork_pa_e_kernel(
 
         identity = keep.tile([P, P], F32)
         make_identity(nc, identity[:])
-        eps = keep.tile([P, 1], F32)
-        nc.vector.memset(eps[:], LN_EPS)
 
         def spread_bias(l):
             for half in range(HALVES):
                 cols = slice(BANK * half, BANK * (half + 1))
                 b_bank = turn_psum.tile([P, BANK], F32, tag="turn", name="b_bank")
                 nc.tensor.matmul(out=b_bank[:], lhsT=pick[:, l, :], rhs=b_rows[:, cols], start=True, stop=True)
-                if l == 0:
-                    nc.vector.tensor_copy(out=b_all[:, l, cols], in_=b_bank[:])
-                else:
-                    nc.scalar.copy(out=b_all[:, l, cols], in_=b_bank[:])
+                nc.scalar.copy(out=b_all[:, l, cols], in_=b_bank[:])
 
         wide = {}
 
         def spread_wide(row):
             for half in range(HALVES):
                 cols = slice(BANK * half, BANK * (half + 1))
-                wide[half] = gain_psum.tile([P, BANK], F32, tag="wide%d" % half, name="wide%d" % half)
+                wide[half] = wide_psum.tile([P, BANK], F32, tag="wide%d" % half, name="wide%d" % half)
                 nc.tensor.matmul(out=wide[half][:], lhsT=pick[:, row, :], rhs=b_rows[:, cols], start=True, stop=True)
 
         h_codes = keep.tile([P, ROW_TILES, PASSES * P], U32, align_bytes=64)
         h_scales = keep.tile([P, ROW_TILES, PASSES * P], U8, align_bytes=64)
+        turned = {}
+        grouped = {}
 
-        def quantise_row_tile(rt):
+        def turn_h(rt):
             pairs = h_sb[:, rt, :].bitcast(F32)
-            turned = turn_psum.tile([P, PASSES, 2, P], F32, tag="turn", name="turned")
+            turned[rt] = turn_psum.tile([P, PASSES, 2, P], F32, tag="turn", name="turned")
             for c in range(PASSES):
                 for u in range(2):
-                    nc.tensor.transpose(
-                        turned[:, c, u, :], pairs[:, 256 * c + u : 256 * (c + 1) : 2], identity[:]
-                    )
-            grouped = blocks.tile([P, PASSES, P, 2], F32, align_bytes=64, name="grouped")
-            nc.scalar.copy(out=grouped[:], in_=turned[:].rearrange("p c u r -> p c r u"))
+                    nc.tensor.transpose(turned[rt][:, c, u, :], pairs[:, 256 * c + u : 256 * (c + 1) : 2], identity[:])
+
+        def group_h(rt):
+            grouped[rt] = blocks.tile([P, PASSES, P, 2], F32, align_bytes=64, name="grouped")
+            nc.scalar.copy(out=grouped[rt][:], in_=turned[rt][:].rearrange("p c u r -> p c r u"))
+
+        def quantise_h(rt):
             nc.vector.quantize_mx(
                 out=h_codes[:, rt, :].bitcast(FP8X4),
                 scales=h_scales[:, rt, :],
-                in_=grouped[:].rearrange("p c r u -> p (c r u)").bitcast(BF16),
+                in_=grouped[rt][:].rearrange("p c r u -> p (c r u)").bitcast(BF16),
             )
 
         h_plus_b = {}
         pre_rows = {}
         z_rows = {}
         total_feat = {}
+        own_feat = {}
         row_sums = {}
         neg_mean = {}
         sum_squares = {}
@@ -146,33 +174,31 @@ def tile_advancedliquidneuralnetwork_pa_e_kernel(
         shift = {}
         result = {}
         gained = {}
+        lin = {}
 
-        def prepare(unit):
+        def where(unit):
             block, r4 = divmod(unit, STEPS)
             grp, l = divmod(block, BRANCHES)
-            rt = GROUP_TILES * grp + r4
-            if l == 0:
-                quantise_row_tile(rt)
-            h_plus_b[unit] = units.tile([P, H], F32, name="h_plus_b")
+            return block, r4, grp, l, GROUP_TILES * grp + r4
+
+        def add_bias(unit):
+            block, r4, grp, l, rt = where(unit)
             if unit in VECTOR_ADDS:
+                h_plus_b[unit] = units.tile([P, H], F32, name="h_plus_b_vector", bufs=BUFS_ADD_V)
                 for half in range(HALVES):
                     cols = slice(BANK * half, BANK * (half + 1))
                     nc.vector.tensor_tensor(out=h_plus_b[unit][:, cols], in0=h_sb[:, rt, cols], in1=wide[half][:], op=ALU.add)
-                return
-            nc.gpsimd.tensor_tensor(out=h_plus_b[unit][:], in0=h_sb[:, rt, :], in1=b_all[:, l, :], op=ALU.add)
+            else:
+                h_plus_b[unit] = units.tile([P, H], F32, name="h_plus_b", bufs=BUFS_ADD_G)
+                nc.gpsimd.tensor_tensor(out=h_plus_b[unit][:], in0=h_sb[:, rt, :], in1=b_all[:, l, :], op=ALU.add)
 
         def product(unit, half):
-            block, r4 = divmod(unit, STEPS)
-            grp, l = divmod(block, BRANCHES)
-            rt = GROUP_TILES * grp + r4
-            if half == 0:
-                pre_rows[unit] = units.tile([P, H], F32, name="pre_rows")
-                row_sums[unit] = stats.tile([P, HALVES], F32, name="row_sums")
-            lin = lin_psum.tile([P, BANK], F32, name="lin")
+            block, r4, grp, l, rt = where(unit)
+            lin[unit, half] = lin_psum.tile([P, BANK], F32, name="lin")
             for c in range(PASSES):
                 chunk = l * PASSES + c
                 nc.tensor.matmul_mx(
-                    out=lin[:],
+                    out=lin[unit, half][:],
                     lhsT=h_codes[:, rt, c * P : (c + 1) * P].bitcast(FP8X4),
                     lhsT_scale=h_scales[:, rt, c * P : (c + 1) * P],
                     rhs=w_words[:, chunk, 2 * BANK * half : 2 * BANK * (half + 1)].bitcast(FP4X4),
@@ -180,10 +206,15 @@ def tile_advancedliquidneuralnetwork_pa_e_kernel(
                     start=(c == 0),
                     stop=(c == PASSES - 1),
                 )
+
+        def collect(unit, half):
+            if half == 0:
+                pre_rows[unit] = units.tile([P, H], F32, name="pre_rows", bufs=BUFS_PRE)
+                row_sums[unit] = stats.tile([P, HALVES], F32, name="row_sums")
             cols = slice(BANK * half, BANK * (half + 1))
             nc.vector.scalar_tensor_tensor(
                 out=pre_rows[unit][:, cols],
-                in0=lin[:],
+                in0=lin[unit, half][:],
                 scalar=1.0,
                 in1=h_plus_b[unit][:, cols],
                 op0=ALU.mult,
@@ -214,7 +245,7 @@ def tile_advancedliquidneuralnetwork_pa_e_kernel(
                 accum_out=sum_squares[unit][:],
             )
 
-        def scale_and_shift(unit):
+        def inverse_std(unit):
             inv_std[unit] = stats.tile([P, 1], F32, name="inv_std")
             nc.scalar.activation(
                 out=inv_std[unit][:],
@@ -223,15 +254,13 @@ def tile_advancedliquidneuralnetwork_pa_e_kernel(
                 bias=eps[:],
                 scale=1.0 / H,
             )
-            if (unit // STEPS) % BRANCHES == BRANCHES - 1 or unit % STEPS == 0:
+            if where(unit)[3] == LAST or unit in GPSIMD_NORMALISES:
                 return
             shift[unit] = stats.tile([P, 1], F32, name="shift")
-            nc.scalar.activation(
-                out=shift[unit][:], in_=neg_mean[unit][:], func=ACT.Identity, scale=inv_std[unit][:]
-            )
+            nc.scalar.activation(out=shift[unit][:], in_=neg_mean[unit][:], func=ACT.Identity, scale=inv_std[unit][:])
 
         def centre_and_gain(unit):
-            gained[unit] = units.tile([P, H], F32, name="gained")
+            gained[unit] = units.tile([P, H], F32, name="gained", bufs=BUFS_GAINED)
             for half in range(HALVES):
                 cols = slice(BANK * half, BANK * (half + 1))
                 nc.vector.scalar_tensor_tensor(
@@ -243,35 +272,11 @@ def tile_advancedliquidneuralnetwork_pa_e_kernel(
                     op1=ALU.mult,
                 )
 
-        def finish_rows(unit, half):
-            block, r4 = divmod(unit, STEPS)
-            grp = block // BRANCHES
-            if half == 0:
-                result[grp] = blocks.tile([P, H], F32, name="result")
-            out_rows = turn_psum.tile([P, BANK], F32, tag="turn", name="out_rows")
-            for q in range(BANK // P):
-                nc.tensor.transpose(
-                    out_rows[:, P * q : P * (q + 1)],
-                    total_feat[grp][:, (BANK // P) * half + q, P * r4 : P * (r4 + 1)],
-                    identity[:],
-                )
-            cols = slice(BANK * half, BANK * (half + 1))
-            nc.vector.scalar_tensor_tensor(
-                out=result[grp][:, cols],
-                in0=gained[unit][:, cols],
-                scalar=inv_std[unit][:],
-                in1=out_rows[:],
-                op0=ALU.mult,
-                op1=ALU.add,
-            )
-            rt = GROUP_TILES * grp + r4
-            nc.sync.dma_start(out=out[rt * P : (rt + 1) * P, cols], in_=result[grp][:, cols])
-
         def normalise(unit):
-            block, r4 = divmod(unit, STEPS)
+            block, r4, grp, l, rt = where(unit)
             if r4 == 0:
                 z_rows[block] = blocks.tile([P, GROUP_TILES, H], F32, name="z_rows")
-            if r4 == 0:
+            if unit in GPSIMD_NORMALISES:
                 nc.gpsimd.tensor_scalar(
                     out=z_rows[block][:, r4, :],
                     in0=pre_rows[unit][:],
@@ -280,14 +285,14 @@ def tile_advancedliquidneuralnetwork_pa_e_kernel(
                     op0=ALU.add,
                     op1=ALU.mult,
                 )
-                return
-            nc.scalar.activation(
-                out=z_rows[block][:, r4, :],
-                in_=pre_rows[unit][:],
-                func=ACT.Identity,
-                bias=shift[unit][:],
-                scale=inv_std[unit][:],
-            )
+            else:
+                nc.scalar.activation(
+                    out=z_rows[block][:, r4, :],
+                    in_=pre_rows[unit][:],
+                    func=ACT.Identity,
+                    bias=shift[unit][:],
+                    scale=inv_std[unit][:],
+                )
 
         vector_columns = keep.tile([P, P], F32)
         beta_sum = keep.tile([P, FEATURE_TILES], F32)
@@ -298,88 +303,134 @@ def tile_advancedliquidneuralnetwork_pa_e_kernel(
             vector_bank = turn_psum.tile([P, P], F32, tag="turn", name="vector_bank")
             nc.tensor.transpose(vector_bank[:], vector_rows_f32[:], identity[:])
             nc.vector.tensor_copy(out=vector_columns[:], in_=vector_bank[:])
-            nc.vector.tensor_tensor(
-                out=beta_sum[:], in0=vector_columns[:, 32:40], in1=vector_columns[:, 40:48], op=ALU.add
-            )
+            nc.vector.tensor_tensor(out=beta_sum[:], in0=vector_columns[:, 32:40], in1=vector_columns[:, 40:48], op=ALU.add)
             nc.vector.tensor_tensor(out=beta_sum[:], in0=beta_sum[:], in1=vector_columns[:, 48:56], op=ALU.add)
 
-        def gain_and_add(block, ft):
+        def gain(block, ft):
             grp, l = divmod(block, BRANCHES)
             if l == 0 and ft == 0:
-                total_feat[grp] = blocks.tile([P, FEATURE_TILES, BANK], F32, name="total_feat")
-            gain = vector_columns[:, FEATURE_TILES * l + ft : FEATURE_TILES * l + ft + 1]
+                total_feat[grp] = blocks.tile([P, FEATURE_TILES, BANK], F32, tag="feat", name="total_feat", bufs=BUFS_FEAT)
+            factor = vector_columns[:, FEATURE_TILES * l + ft : FEATURE_TILES * l + ft + 1]
             z_feat = turn_psum.tile([P, BANK], F32, tag="turn", name="z_feat")
             for r4 in range(GROUP_TILES):
-                nc.tensor.transpose(
-                    z_feat[:, P * r4 : P * (r4 + 1)], z_rows[block][:, r4, P * ft : P * (ft + 1)], identity[:]
+                nc.tensor.transpose(z_feat[:, P * r4 : P * (r4 + 1)], z_rows[block][:, r4, P * ft : P * (ft + 1)], identity[:])
+            if l == 0 and (block, ft) in VECTOR_FIRST:
+                nc.vector.tensor_scalar(
+                    out=total_feat[grp][:, ft, :], in0=z_feat[:], scalar1=factor, scalar2=beta_sum[:, ft : ft + 1], op0=ALU.mult, op1=ALU.add
                 )
-            if l == 0:
+            elif l == 0:
                 nc.scalar.activation(
-                    out=total_feat[grp][:, ft, :],
-                    in_=z_feat[:],
-                    func=ACT.Identity,
-                    bias=beta_sum[:, ft : ft + 1],
-                    scale=gain,
+                    out=total_feat[grp][:, ft, :], in_=z_feat[:], func=ACT.Identity, bias=beta_sum[:, ft : ft + 1], scale=factor
                 )
+            elif (block, ft) in OWN_TILES:
+                if grp not in own_feat:
+                    own_feat[grp] = blocks.tile([P, FEATURE_TILES, BANK], F32, tag="feat", name="own_feat", bufs=BUFS_FEAT)
+                nc.scalar.activation(out=own_feat[grp][:, ft, :], in_=z_feat[:], func=ACT.Identity, scale=factor)
             else:
                 nc.vector.scalar_tensor_tensor(
                     out=total_feat[grp][:, ft, :],
                     in0=z_feat[:],
-                    scalar=gain,
+                    scalar=factor,
                     in1=total_feat[grp][:, ft, :],
                     op0=ALU.mult,
                     op1=ALU.add,
                 )
 
-        def finish(grp, r4, half):
+        def finish(unit, half):
+            block, r4, grp, l, rt = where(unit)
             if half == 0:
                 result[grp] = blocks.tile([P, H], F32, name="result")
             out_rows = turn_psum.tile([P, BANK], F32, tag="turn", name="out_rows")
             for q in range(BANK // P):
-                nc.tensor.transpose(
-                    out_rows[:, P * q : P * (q + 1)],
-                    total_feat[grp][:, (BANK // P) * half + q, P * r4 : P * (r4 + 1)],
-                    identity[:],
-                )
+                ft = (BANK // P) * half + q
+                parts = [total_feat[grp]] + ([own_feat[grp]] if (block - 1, ft) in OWN_TILES else [])
+                for i, part in enumerate(parts):
+                    nc.tensor.matmul(
+                        out=out_rows[:, P * q : P * (q + 1)],
+                        lhsT=part[:, ft, P * r4 : P * (r4 + 1)],
+                        rhs=identity[:],
+                        is_transpose=True,
+                        start=(i == 0),
+                        stop=(i == len(parts) - 1),
+                    )
             cols = slice(BANK * half, BANK * (half + 1))
-            if half == 0:
-                nc.scalar.copy(out=result[grp][:, cols], in_=out_rows[:])
-            else:
-                nc.vector.tensor_copy(out=result[grp][:, cols], in_=out_rows[:])
-                rt = GROUP_TILES * grp + r4
-                nc.sync.dma_start(out=out[rt * P : (rt + 1) * P, :], in_=result[grp][:])
+            nc.vector.scalar_tensor_tensor(
+                out=result[grp][:, cols],
+                in0=gained[unit][:, cols],
+                scalar=inv_std[unit][:],
+                in1=out_rows[:],
+                op0=ALU.mult,
+                op1=ALU.add,
+            )
+            nc.sync.dma_start(out=out[rt * P : (rt + 1) * P, cols], in_=result[grp][:, cols])
 
-        product_at = LAG_PRODUCT
-        statistics_at = product_at + LAG_STATISTICS
-        normalise_at = statistics_at + LAG_NORMALISE
-        back_at = normalise_at + LAG_BACK
-        all_steps = BLOCKS * STEPS
-        for now in range(all_steps + back_at + STEPS):
-            if now < BRANCHES:
-                spread_bias(now)
-            if now % STEPS == 0 and now // STEPS < BRANCHES:
-                spread_wide((0, 1, BRANCHES)[now // STEPS])
-            if now < all_steps:
-                prepare(now)
-            if now == LAG_PRODUCT:
-                vectors_to_columns()
-            if 0 <= now - statistics_at < all_steps:
-                square(now - statistics_at)
-                if ((now - statistics_at) // STEPS) % BRANCHES == BRANCHES - 1:
-                    centre_and_gain(now - statistics_at)
-            if 0 <= now - normalise_at < all_steps and ((now - normalise_at) // STEPS) % BRANCHES < BRANCHES - 1:
-                normalise(now - normalise_at)
-            if 0 <= now - statistics_at < all_steps:
-                scale_and_shift(now - statistics_at)
-            if 0 <= now - product_at < all_steps:
-                for half in range(HALVES):
-                    product(now - product_at, half)
-            block, step = divmod(now - back_at, STEPS)
-            if 0 <= block < BLOCKS and block % BRANCHES < BRANCHES - 1:
-                for half in range(HALVES):
-                    gain_and_add(block, HALVES * step + half)
-            if 0 <= block < BLOCKS and block % BRANCHES == BRANCHES - 1:
-                for half in range(HALVES):
-                    finish_rows(STEPS * block + step, half)
-            if 0 <= now - product_at < all_steps:
-                mean(now - product_at)
+        back = {}
+        gains_end = {}
+        for block in range(BLOCKS):
+            grp, l = divmod(block, BRANCHES)
+            last_product = LEAD + STEPS * block + STEPS - 1
+            if l < LAST:
+                for ft in range(FEATURE_TILES):
+                    step = last_product + LAG_GAIN + ft // GAINS_A_STEP[block]
+                    back.setdefault(step, []).append(("gain", block, ft))
+                    gains_end[grp] = step
+            else:
+                for r4 in range(STEPS):
+                    unit = STEPS * block + r4
+                    step = max(LEAD + unit + LAG_FINISH, gains_end[grp] + 1 + r4 // FINISHES_A_STEP[grp])
+                    for half in range(HALVES):
+                        back.setdefault(step, []).append(("finish", unit, half))
+        last_step = max(back)
+
+        if PIN:
+            ctx.enter_context(tc.manual_schedule())
+
+        plan = {}
+
+        def at(key, step, what):
+            plan.setdefault((max(step, 0), key), []).append(what)
+
+        wide_rows = {0: 0, STEPS: 1, 2 * STEPS: BRANCHES}
+        for unit in range(UNITS):
+            block, r4, grp, l, rt = where(unit)
+            here = unit + LEAD
+            at("p", here, unit)
+            at("c", here, unit)
+            at("m", here, unit)
+            at("s", here + LAG_SQUARE, unit)
+            at("i", here + LAG_SQUARE, unit)
+            if l == 0:
+                at("t", here - LAG_TURN[grp], rt)
+                at("g", here - LAG_GROUP[grp], rt)
+                at("q", here - LAG_QUANT[grp], rt)
+            if unit in wide_rows:
+                at("w", here - LAG_ADD_V, wide_rows[unit])
+            if unit in VECTOR_ADDS:
+                at("v", here - LAG_ADD_V, unit)
+            else:
+                at("a", here - LAG_ADD_G, unit)
+            if l < LAST:
+                at("n", here + LAG_NORMALISE, unit)
+            else:
+                at("r", here + LAG_CENTRE, unit)
+        for l in range(BRANCHES):
+            at("f", SPREAD_AT[l], l)
+        at("k", COLUMNS_AT, 0)
+        stage = {"t": turn_h, "g": group_h, "q": quantise_h, "w": spread_wide, "v": add_bias, "a": add_bias, "m": mean, "s": square,
+                 "i": inverse_std, "n": normalise, "r": centre_and_gain, "f": spread_bias}
+        for step in range(last_step + 1):
+            for key in ORDER:
+                for what in plan.get((step, key), []):
+                    if key in "pc":
+                        for half in range(HALVES):
+                            (product if key == "p" else collect)(what, half)
+                    elif key == "k":
+                        vectors_to_columns()
+                    else:
+                        stage[key](what)
+                if key == "b":
+                    for job in back.get(step, []):
+                        if job[0] == "gain":
+                            gain(job[1], job[2])
+                        else:
+                            finish(job[1], job[2])

@@ -36,30 +36,30 @@ FLOPS = 2 * BRANCHES * ROWS * H * H
 LEAD = 3
 LAG_TURN = (4, 4)
 LAG_GROUP = (4, 4)
-LAG_QUANT = (3, 2)
-LAG_ADD_V = 4
-LAG_ADD_G = 3
-LAG_SQUARE = 2
-LAG_CENTRE = 0
+LAG_QUANT = (2, 3)
+LAG_ADD_V = 2
+LAG_ADD_G = 4
+LAG_SQUARE = 1
+LAG_CENTRE = 1
 LAG_NORMALISE = 2
 LAG_GAIN = 3
-LAG_FINISH = 0
-VECTOR_ADDS = (0, 4, 5)
-GPSIMD_NORMALISES = (4, 5, 6, 16, 17)
-OWN_TILES = ((1, 4), (1, 5), (1, 6), (1, 7), (4, 4), (4, 5), (4, 6), (4, 7))
-VECTOR_FIRST = ((0, 0), (0, 1), (3, 0))
+LAG_FINISH = 5
+VECTOR_ADDS = (0, 1, 4, 5)
+GPSIMD_NORMALISES = (0, 4, 5, 12, 16, 17)
+OWN_TILES = ((1, 1), (1, 2), (1, 3), (1, 4), (1, 5), (1, 6), (1, 7), (4, 3), (4, 4), (4, 5), (4, 6), (4, 7))
+VECTOR_FIRST = ((0, 0), (0, 1), (0, 2), (0, 3), (0, 4), (3, 0), (3, 1), (3, 2))
 GAINS_A_STEP = (2, 2, 0, 2, 4, 0)
-FINISHES_A_STEP = (1, 1)
-BUFS_ADD_G = 4
+FINISHES_A_STEP = (1, 2)
+BUFS_ADD_G = 6
 BUFS_ADD_V = 2
 BUFS_PRE = 6
-BUFS_GAINED = 7
+BUFS_GAINED = 5
 BUFS_FEAT = 3
 PIN = True
 WARM = True
-ORDER = "pfstwacinmkgqrvb"
-SPREAD_AT = (0, 1, 3)
-COLUMNS_AT = 0
+ORDER = "spwncqfrtagmbvkih"
+SPREAD_AT = (1, 1, 3)
+COLUMNS_AT = 4
 LOADS = "h0 h1 w0 h2 h3 w1 w2 h4 h5 h6 h7"
 
 
@@ -254,8 +254,8 @@ def tile_advancedliquidneuralnetwork_pa_e_kernel(
                 bias=eps[:],
                 scale=1.0 / H,
             )
-            if where(unit)[3] == LAST or unit in GPSIMD_NORMALISES:
-                return
+
+        def make_shift(unit):
             shift[unit] = stats.tile([P, 1], F32, name="shift")
             nc.scalar.activation(out=shift[unit][:], in_=neg_mean[unit][:], func=ACT.Identity, scale=inv_std[unit][:])
 
@@ -399,6 +399,8 @@ def tile_advancedliquidneuralnetwork_pa_e_kernel(
             at("m", here, unit)
             at("s", here + LAG_SQUARE, unit)
             at("i", here + LAG_SQUARE, unit)
+            if l < LAST and unit not in GPSIMD_NORMALISES:
+                at("h", here + LAG_SQUARE, unit)
             if l == 0:
                 at("t", here - LAG_TURN[grp], rt)
                 at("g", here - LAG_GROUP[grp], rt)
@@ -417,7 +419,7 @@ def tile_advancedliquidneuralnetwork_pa_e_kernel(
             at("f", SPREAD_AT[l], l)
         at("k", COLUMNS_AT, 0)
         stage = {"t": turn_h, "g": group_h, "q": quantise_h, "w": spread_wide, "v": add_bias, "a": add_bias, "m": mean, "s": square,
-                 "i": inverse_std, "n": normalise, "r": centre_and_gain, "f": spread_bias}
+                 "i": inverse_std, "h": make_shift, "n": normalise, "r": centre_and_gain, "f": spread_bias}
         for step in range(last_step + 1):
             for key in ORDER:
                 for what in plan.get((step, key), []):

@@ -36,30 +36,34 @@ FLOPS = 2 * BRANCHES * ROWS * H * H
 LEAD = 3
 LAG_TURN = (4, 4)
 LAG_GROUP = (4, 4)
-LAG_QUANT = (2, 3)
+LAG_QUANT = (2, 2)
 LAG_ADD_V = 2
 LAG_ADD_G = 4
-LAG_SQUARE = 1
+LAG_MEAN = 1
+LAG_SQUARE = 2
+LAG_INVERSE = 2
+LAG_SHIFT = 3
+BUFS_RESULT = 3
 LAG_CENTRE = 1
-LAG_NORMALISE = 2
-LAG_GAIN = 3
-LAG_FINISH = 5
+LAG_NORMALISE = 3
+LAG_GAIN = 4
+LAG_FINISH = 8
 VECTOR_ADDS = (0, 1, 4, 5)
-GPSIMD_NORMALISES = (0, 4, 5, 12, 16, 17)
-OWN_TILES = ((1, 1), (1, 2), (1, 3), (1, 4), (1, 5), (1, 6), (1, 7), (4, 3), (4, 4), (4, 5), (4, 6), (4, 7))
-VECTOR_FIRST = ((0, 0), (0, 1), (0, 2), (0, 3), (0, 4), (3, 0), (3, 1), (3, 2))
+GPSIMD_NORMALISES = (0, 1, 4, 5, 12, 16, 17, 18)
+OWN_TILES = ((1, 2), (1, 3), (1, 4), (1, 5), (1, 6), (1, 7), (4, 4), (4, 5), (4, 6), (4, 7))
+VECTOR_FIRST = ((0, 0), (0, 1), (0, 2), (0, 3), (0, 4), (3, 0), (3, 1))
 GAINS_A_STEP = (2, 2, 0, 2, 4, 0)
-FINISHES_A_STEP = (1, 2)
-BUFS_ADD_G = 6
+FINISHES_A_STEP = (2, 2)
+BUFS_ADD_G = 4
 BUFS_ADD_V = 2
-BUFS_PRE = 6
-BUFS_GAINED = 5
+BUFS_PRE = 7
+BUFS_GAINED = 4
 BUFS_FEAT = 3
 PIN = True
 WARM = True
-ORDER = "spwncqfrtagmbvkih"
-SPREAD_AT = (1, 1, 3)
-COLUMNS_AT = 4
+ORDER = "hpscmdfnwaqtgrkbvi"
+SPREAD_AT = (1, 3, 5)
+COLUMNS_AT = 9
 LOADS = "h0 h1 w0 h2 h3 w1 w2 h4 h5 h6 h7"
 
 
@@ -339,7 +343,7 @@ def tile_advancedliquidneuralnetwork_pa_e_kernel(
         def finish(unit, half):
             block, r4, grp, l, rt = where(unit)
             if half == 0:
-                result[grp] = blocks.tile([P, H], F32, name="result")
+                result[grp] = blocks.tile([P, H], F32, name="result", bufs=BUFS_RESULT)
             out_rows = turn_psum.tile([P, BANK], F32, tag="turn", name="out_rows")
             for q in range(BANK // P):
                 ft = (BANK // P) * half + q
@@ -396,11 +400,12 @@ def tile_advancedliquidneuralnetwork_pa_e_kernel(
             here = unit + LEAD
             at("p", here, unit)
             at("c", here, unit)
-            at("m", here, unit)
+            at("d", here, unit)
+            at("m", here + LAG_MEAN, unit)
             at("s", here + LAG_SQUARE, unit)
-            at("i", here + LAG_SQUARE, unit)
+            at("i", here + LAG_INVERSE, unit)
             if l < LAST and unit not in GPSIMD_NORMALISES:
-                at("h", here + LAG_SQUARE, unit)
+                at("h", here + LAG_SHIFT, unit)
             if l == 0:
                 at("t", here - LAG_TURN[grp], rt)
                 at("g", here - LAG_GROUP[grp], rt)
@@ -423,9 +428,11 @@ def tile_advancedliquidneuralnetwork_pa_e_kernel(
         for step in range(last_step + 1):
             for key in ORDER:
                 for what in plan.get((step, key), []):
-                    if key in "pc":
+                    if key == "p":
                         for half in range(HALVES):
-                            (product if key == "p" else collect)(what, half)
+                            product(what, half)
+                    elif key in "cd":
+                        collect(what, "cd".index(key))
                     elif key == "k":
                         vectors_to_columns()
                     else:

@@ -36,9 +36,9 @@ FLOPS = 2 * BRANCHES * ROWS * H * H
 LEAD = 3
 LAG_TURN = (4, 4)
 LAG_GROUP = (4, 4)
-LAG_QUANT = (2, 2)
+LAG_QUANT = (3, 2)
 LAG_ADD_V = 2
-LAG_ADD_G = 4
+LAG_ADD_G = 3
 LAG_MEAN = 1
 LAG_SQUARE = 2
 LAG_INVERSE = 2
@@ -47,22 +47,22 @@ BUFS_RESULT = 3
 LAG_CENTRE = 1
 LAG_NORMALISE = 3
 LAG_GAIN = 4
-LAG_FINISH = 8
+LAG_FINISH = 5
 VECTOR_ADDS = (0, 1, 4, 5)
-GPSIMD_NORMALISES = (0, 1, 4, 5, 12, 16, 17, 18)
+GPSIMD_NORMALISES = (4, 5, 16, 17, 18)
 OWN_TILES = ((1, 2), (1, 3), (1, 4), (1, 5), (1, 6), (1, 7), (4, 4), (4, 5), (4, 6), (4, 7))
-VECTOR_FIRST = ((0, 0), (0, 1), (0, 2), (0, 3), (0, 4), (3, 0), (3, 1))
+VECTOR_FIRST = ((0, 0), (0, 1), (0, 2), (0, 3), (3, 0), (3, 1))
 GAINS_A_STEP = (2, 2, 0, 2, 4, 0)
-FINISHES_A_STEP = (2, 2)
+FINISHES_A_STEP = (4, 1)
 BUFS_ADD_G = 4
-BUFS_ADD_V = 2
+BUFS_ADD_V = 3
 BUFS_PRE = 7
 BUFS_GAINED = 4
 BUFS_FEAT = 3
 PIN = True
 WARM = True
-ORDER = "hpscmdfnwaqtgrkbvi"
-SPREAD_AT = (1, 3, 5)
+ORDER = "pahsmfwcnktdgrqbvi"
+SPREAD_AT = (1, 3, 2)
 COLUMNS_AT = 9
 LOADS = "h0 h1 w0 h2 h3 w1 w2 h4 h5 h6 h7"
 

from contextlib import ExitStack

import concourse.mybir as mybir
from concourse.masks import make_identity

F32 = mybir.dt.float32
BF16 = mybir.dt.bfloat16
I32 = mybir.dt.int32
U32 = mybir.dt.uint32
U8 = mybir.dt.uint8
FP8X4 = mybir.dt.float8_e4m3fn_x4
FP4X4 = mybir.dt.float4_e2m1fn_x4
ALU = mybir.AluOpType
ACT = mybir.ActivationFunctionType

P = 128
ROWS = 1024
H = 1024
BRANCHES = 3
LN_EPS = 1e-5
K_PASS = 4 * P
PASSES = H // K_PASS
BANK = 512
GROUP_TILES = BANK // P
GROUPS = ROWS // BANK
FEATURE_TILES = H // P
HALVES = H // BANK
BLOCKS = GROUPS * BRANCHES
STEPS = GROUP_TILES
ROW_TILES = GROUPS * GROUP_TILES
UNITS = BLOCKS * STEPS
LAST = BRANCHES - 1

FLOPS = 2 * BRANCHES * ROWS * H * H

LEAD = 3
LAG_TURN = (4, 4)
LAG_GROUP = (4, 4)
LAG_QUANT = (3, 2)
LAG_ADD_V = 2
LAG_ADD_G = 3
LAG_MEAN = 1
LAG_SQUARE = 2
LAG_INVERSE = 2
LAG_SHIFT = 3
BUFS_RESULT = 3
LAG_CENTRE = 1
LAG_NORMALISE = 3
LAG_GAIN = 4
LAG_FINISH = 5
VECTOR_ADDS = (0, 1, 4, 5)
GPSIMD_NORMALISES = (4, 5, 16, 17, 18)
OWN_TILES = ((1, 2), (1, 3), (1, 4), (1, 5), (1, 6), (1, 7), (4, 4), (4, 5), (4, 6), (4, 7))
VECTOR_FIRST = ((0, 0), (0, 1), (0, 2), (0, 3), (3, 0), (3, 1))
GAINS_A_STEP = (2, 2, 0, 2, 4, 0)
FINISHES_A_STEP = (4, 1)
BUFS_ADD_G = 4
BUFS_ADD_V = 3
BUFS_PRE = 7
BUFS_GAINED = 4
BUFS_FEAT = 3
PIN = True
WARM = True
ORDER = "pahsmfwcnktdgrqbvi"
SPREAD_AT = (1, 3, 2)
COLUMNS_AT = 9
LOADS = "h0 h1 w0 h2 h3 w1 w2 h4 h5 h6 h7"


def tile_advancedliquidneuralnetwork_pa_e_kernel(
    tc, h, W_liq_words, W_liq_scales, b_liq, g_liq, beta_liq, out
):
    nc = tc.nc
    with ExitStack() as ctx:
        keep = ctx.enter_context(tc.tile_pool(name="keep", bufs=1))
        blocks = ctx.enter_context(tc.tile_pool(name="blocks", bufs=2))
        units = ctx.enter_context(tc.tile_pool(name="units", bufs=4))
        stats = ctx.enter_context(tc.tile_pool(name="stats", bufs=8))
        lin_psum = ctx.enter_context(tc.psum_pool(name="lin_psum", bufs=3))
        turn_psum = ctx.enter_context(tc.psum_pool(name="turn_psum", bufs=3))
        wide_psum = ctx.enter_context(tc.psum_pool(name="wide_psum", bufs=1))

        h_sb = keep.tile([P, ROW_TILES, H], BF16)
        w_words = keep.tile([P, BRANCHES * PASSES, 2 * H], U8, align_bytes=64)
        w_scales = keep.tile([P, BRANCHES * PASSES, H], U8, align_bytes=64)
        for l in range(BRANCHES):
            nc.vector.memset(w_scales[:, PASSES * l : PASSES * (l + 1), :].bitcast(I32), 0)
        vector_rows = keep.tile([P, P], BF16)
        nc.vector.memset(vector_rows[:], 0.0)
        b_all = keep.tile([P, BRANCHES, H], BF16)
        b_rows = keep.tile([P, H], BF16)
        nc.gpsimd.memset(b_rows[:].bitcast(F32), 0.0)
        pick = keep.tile([P, BRANCHES + 1, P], BF16)
        nc.gpsimd.memset(pick[:], 0.0)
        for l in range(BRANCHES):
            nc.gpsimd.memset(pick[32 * l : 32 * l + 1, l, :], 1.0)
            nc.scalar.dma_start(out=b_rows[32 * l : 32 * l + 1, :], in_=b_liq[l : l + 1, :])
        nc.gpsimd.memset(pick[96:97, BRANCHES, :], 1.0)
        nc.scalar.dma_start(out=b_rows[96:97, :], in_=g_liq[LAST : LAST + 1, :])
        eps = keep.tile([P, 1], F32)
        nc.vector.memset(eps[:], LN_EPS)
        if WARM:
            warm = keep.tile([P, 1], F32)
            nc.scalar.activation(out=warm[:], in_=eps[:], func=ACT.Abs_reciprocal_sqrt, bias=eps[:], scale=1.0)

        def load_weights(l):
            chunks = slice(PASSES * l, PASSES * (l + 1))
            for quad in range(4):
                nc.sync.dma_start(
                    out=w_scales[32 * quad : 32 * quad + 4, chunks, :].bitcast(I32),
                    in_=W_liq_scales[chunks, 4 * quad : 4 * quad + 4, :].rearrange("c r n -> r c n").bitcast(I32),
                )
            for chunk in range(PASSES * l, PASSES * (l + 1)):
                nc.sync.dma_start(out=w_words[:, chunk, :].bitcast(I32), in_=W_liq_words[chunk].bitcast(I32))

        for item in LOADS.split(" "):
            number = int(item[1:])
            if item[0] == "h":
                nc.sync.dma_start(out=h_sb[:, number, :], in_=h[number * P : (number + 1) * P, :])
            else:
                load_weights(number)
        for kind, vectors in enumerate((g_liq, beta_liq)):
            nc.scalar.dma_start(
                out=vector_rows[32 * kind : 32 * kind + BRANCHES * FEATURE_TILES, :],
                in_=vectors.rearrange("l (ft p) -> (l ft) p", p=P),
            )

        identity = keep.tile([P, P], F32)
        make_identity(nc, identity[:])

        def spread_bias(l):
            for half in range(HALVES):
                cols = slice(BANK * half, BANK * (half + 1))
                b_bank = turn_psum.tile([P, BANK], F32, tag="turn", name="b_bank")
                nc.tensor.matmul(out=b_bank[:], lhsT=pick[:, l, :], rhs=b_rows[:, cols], start=True, stop=True)
                nc.scalar.copy(out=b_all[:, l, cols], in_=b_bank[:])

        wide = {}

        def spread_wide(row):
            for half in range(HALVES):
                cols = slice(BANK * half, BANK * (half + 1))
                wide[half] = wide_psum.tile([P, BANK], F32, tag="wide%d" % half, name="wide%d" % half)
                nc.tensor.matmul(out=wide[half][:], lhsT=pick[:, row, :], rhs=b_rows[:, cols], start=True, stop=True)

        h_codes = keep.tile([P, ROW_TILES, PASSES * P], U32, align_bytes=64)
        h_scales = keep.tile([P, ROW_TILES, PASSES * P], U8, align_bytes=64)
        turned = {}
        grouped = {}

        def turn_h(rt):
            pairs = h_sb[:, rt, :].bitcast(F32)
            turned[rt] = turn_psum.tile([P, PASSES, 2, P], F32, tag="turn", name="turned")
            for c in range(PASSES):
                for u in range(2):
                    nc.tensor.transpose(turned[rt][:, c, u, :], pairs[:, 256 * c + u : 256 * (c + 1) : 2], identity[:])

        def group_h(rt):
            grouped[rt] = blocks.tile([P, PASSES, P, 2], F32, align_bytes=64, name="grouped")
            nc.scalar.copy(out=grouped[rt][:], in_=turned[rt][:].rearrange("p c u r -> p c r u"))

        def quantise_h(rt):
            nc.vector.quantize_mx(
                out=h_codes[:, rt, :].bitcast(FP8X4),
                scales=h_scales[:, rt, :],
                in_=grouped[rt][:].rearrange("p c r u -> p (c r u)").bitcast(BF16),
            )

        h_plus_b = {}
        pre_rows = {}
        z_rows = {}
        total_feat = {}
        own_feat = {}
        row_sums = {}
        neg_mean = {}
        sum_squares = {}
        inv_std = {}
        shift = {}
        result = {}
        gained = {}
        lin = {}

        def where(unit):
            block, r4 = divmod(unit, STEPS)
            grp, l = divmod(block, BRANCHES)
            return block, r4, grp, l, GROUP_TILES * grp + r4

        def add_bias(unit):
            block, r4, grp, l, rt = where(unit)
            if unit in VECTOR_ADDS:
                h_plus_b[unit] = units.tile([P, H], F32, name="h_plus_b_vector", bufs=BUFS_ADD_V)
                for half in range(HALVES):
                    cols = slice(BANK * half, BANK * (half + 1))
                    nc.vector.tensor_tensor(out=h_plus_b[unit][:, cols], in0=h_sb[:, rt, cols], in1=wide[half][:], op=ALU.add)
            else:
                h_plus_b[unit] = units.tile([P, H], F32, name="h_plus_b", bufs=BUFS_ADD_G)
                nc.gpsimd.tensor_tensor(out=h_plus_b[unit][:], in0=h_sb[:, rt, :], in1=b_all[:, l, :], op=ALU.add)

        def product(unit, half):
            block, r4, grp, l, rt = where(unit)
            lin[unit, half] = lin_psum.tile([P, BANK], F32, name="lin")
            for c in range(PASSES):
                chunk = l * PASSES + c
                nc.tensor.matmul_mx(
                    out=lin[unit, half][:],
                    lhsT=h_codes[:, rt, c * P : (c + 1) * P].bitcast(FP8X4),
                    lhsT_scale=h_scales[:, rt, c * P : (c + 1) * P],
                    rhs=w_words[:, chunk, 2 * BANK * half : 2 * BANK * (half + 1)].bitcast(FP4X4),
                    rhs_scale=w_scales[:, chunk, BANK * half : BANK * (half + 1)],
                    start=(c == 0),
                    stop=(c == PASSES - 1),
                )

        def collect(unit, half):
            if half == 0:
                pre_rows[unit] = units.tile([P, H], F32, name="pre_rows", bufs=BUFS_PRE)
                row_sums[unit] = stats.tile([P, HALVES], F32, name="row_sums")
            cols = slice(BANK * half, BANK * (half + 1))
            nc.vector.scalar_tensor_tensor(
                out=pre_rows[unit][:, cols],
                in0=lin[unit, half][:],
                scalar=1.0,
                in1=h_plus_b[unit][:, cols],
                op0=ALU.mult,
                op1=ALU.add,
                accum_out=row_sums[unit][:, half : half + 1],
            )

        def mean(unit):
            neg_mean[unit] = stats.tile([P, 1], F32, name="neg_mean")
            nc.vector.tensor_scalar(
                out=neg_mean[unit][:],
                in0=row_sums[unit][:, 0:1],
                scalar1=row_sums[unit][:, 1:2],
                scalar2=-1.0 / H,
                op0=ALU.add,
                op1=ALU.mult,
            )

        def square(unit):
            squares = blocks.tile([P, H], BF16, name="squares")
            sum_squares[unit] = stats.tile([P, 1], F32, name="sum_squares")
            nc.scalar.activation(
                out=squares[:],
                in_=pre_rows[unit][:],
                func=ACT.Square,
                bias=neg_mean[unit][:],
                scale=1.0,
                accum_out=sum_squares[unit][:],
            )

        def inverse_std(unit):
            inv_std[unit] = stats.tile([P, 1], F32, name="inv_std")
            nc.scalar.activation(
                out=inv_std[unit][:],
                in_=sum_squares[unit][:],
                func=ACT.Abs_reciprocal_sqrt,
                bias=eps[:],
                scale=1.0 / H,
            )

        def make_shift(unit):
            shift[unit] = stats.tile([P, 1], F32, name="shift")
            nc.scalar.activation(out=shift[unit][:], in_=neg_mean[unit][:], func=ACT.Identity, scale=inv_std[unit][:])

        def centre_and_gain(unit):
            gained[unit] = units.tile([P, H], F32, name="gained", bufs=BUFS_GAINED)
            for half in range(HALVES):
                cols = slice(BANK * half, BANK * (half + 1))
                nc.vector.scalar_tensor_tensor(
                    out=gained[unit][:, cols],
                    in0=pre_rows[unit][:, cols],
                    scalar=neg_mean[unit][:],
                    in1=wide[half][:],
                    op0=ALU.add,
                    op1=ALU.mult,
                )

        def normalise(unit):
            block, r4, grp, l, rt = where(unit)
            if r4 == 0:
                z_rows[block] = blocks.tile([P, GROUP_TILES, H], F32, name="z_rows")
            if unit in GPSIMD_NORMALISES:
                nc.gpsimd.tensor_scalar(
                    out=z_rows[block][:, r4, :],
                    in0=pre_rows[unit][:],
                    scalar1=neg_mean[unit][:],
                    scalar2=inv_std[unit][:],
                    op0=ALU.add,
                    op1=ALU.mult,
                )
            else:
                nc.scalar.activation(
                    out=z_rows[block][:, r4, :],
                    in_=pre_rows[unit][:],
                    func=ACT.Identity,
                    bias=shift[unit][:],
                    scale=inv_std[unit][:],
                )

        vector_columns = keep.tile([P, P], F32)
        beta_sum = keep.tile([P, FEATURE_TILES], F32)

        def vectors_to_columns():
            vector_rows_f32 = keep.tile([P, P], F32, name="vector_rows_f32")
            nc.vector.tensor_copy(out=vector_rows_f32[:], in_=vector_rows[:])
            vector_bank = turn_psum.tile([P, P], F32, tag="turn", name="vector_bank")
            nc.tensor.transpose(vector_bank[:], vector_rows_f32[:], identity[:])
            nc.vector.tensor_copy(out=vector_columns[:], in_=vector_bank[:])
            nc.vector.tensor_tensor(out=beta_sum[:], in0=vector_columns[:, 32:40], in1=vector_columns[:, 40:48], op=ALU.add)
            nc.vector.tensor_tensor(out=beta_sum[:], in0=beta_sum[:], in1=vector_columns[:, 48:56], op=ALU.add)

        def gain(block, ft):
            grp, l = divmod(block, BRANCHES)
            if l == 0 and ft == 0:
                total_feat[grp] = blocks.tile([P, FEATURE_TILES, BANK], F32, tag="feat", name="total_feat", bufs=BUFS_FEAT)
            factor = vector_columns[:, FEATURE_TILES * l + ft : FEATURE_TILES * l + ft + 1]
            z_feat = turn_psum.tile([P, BANK], F32, tag="turn", name="z_feat")
            for r4 in range(GROUP_TILES):
                nc.tensor.transpose(z_feat[:, P * r4 : P * (r4 + 1)], z_rows[block][:, r4, P * ft : P * (ft + 1)], identity[:])
            if l == 0 and (block, ft) in VECTOR_FIRST:
                nc.vector.tensor_scalar(
                    out=total_feat[grp][:, ft, :], in0=z_feat[:], scalar1=factor, scalar2=beta_sum[:, ft : ft + 1], op0=ALU.mult, op1=ALU.add
                )
            elif l == 0:
                nc.scalar.activation(
                    out=total_feat[grp][:, ft, :], in_=z_feat[:], func=ACT.Identity, bias=beta_sum[:, ft : ft + 1], scale=factor
                )
            elif (block, ft) in OWN_TILES:
                if grp not in own_feat:
                    own_feat[grp] = blocks.tile([P, FEATURE_TILES, BANK], F32, tag="feat", name="own_feat", bufs=BUFS_FEAT)
                nc.scalar.activation(out=own_feat[grp][:, ft, :], in_=z_feat[:], func=ACT.Identity, scale=factor)
            else:
                nc.vector.scalar_tensor_tensor(
                    out=total_feat[grp][:, ft, :],
                    in0=z_feat[:],
                    scalar=factor,
                    in1=total_feat[grp][:, ft, :],
                    op0=ALU.mult,
                    op1=ALU.add,
                )

        def finish(unit, half):
            block, r4, grp, l, rt = where(unit)
            if half == 0:
                result[grp] = blocks.tile([P, H], F32, name="result", bufs=BUFS_RESULT)
            out_rows = turn_psum.tile([P, BANK], F32, tag="turn", name="out_rows")
            for q in range(BANK // P):
                ft = (BANK // P) * half + q
                parts = [total_feat[grp]] + ([own_feat[grp]] if (block - 1, ft) in OWN_TILES else [])
                for i, part in enumerate(parts):
                    nc.tensor.matmul(
                        out=out_rows[:, P * q : P * (q + 1)],
                        lhsT=part[:, ft, P * r4 : P * (r4 + 1)],
                        rhs=identity[:],
                        is_transpose=True,
                        start=(i == 0),
                        stop=(i == len(parts) - 1),
                    )
            cols = slice(BANK * half, BANK * (half + 1))
            nc.vector.scalar_tensor_tensor(
                out=result[grp][:, cols],
                in0=gained[unit][:, cols],
                scalar=inv_std[unit][:],
                in1=out_rows[:],
                op0=ALU.mult,
                op1=ALU.add,
            )
            nc.sync.dma_start(out=out[rt * P : (rt + 1) * P, cols], in_=result[grp][:, cols])

        back = {}
        gains_end = {}
        for block in range(BLOCKS):
            grp, l = divmod(block, BRANCHES)
            last_product = LEAD + STEPS * block + STEPS - 1
            if l < LAST:
                for ft in range(FEATURE_TILES):
                    step = last_product + LAG_GAIN + ft // GAINS_A_STEP[block]
                    back.setdefault(step, []).append(("gain", block, ft))
                    gains_end[grp] = step
            else:
                for r4 in range(STEPS):
                    unit = STEPS * block + r4
                    step = max(LEAD + unit + LAG_FINISH, gains_end[grp] + 1 + r4 // FINISHES_A_STEP[grp])
                    for half in range(HALVES):
                        back.setdefault(step, []).append(("finish", unit, half))
        last_step = max(back)

        if PIN:
            ctx.enter_context(tc.manual_schedule())

        plan = {}

        def at(key, step, what):
            plan.setdefault((max(step, 0), key), []).append(what)

        wide_rows = {0: 0, STEPS: 1, 2 * STEPS: BRANCHES}
        for unit in range(UNITS):
            block, r4, grp, l, rt = where(unit)
            here = unit + LEAD
            at("p", here, unit)
            at("c", here, unit)
            at("d", here, unit)
            at("m", here + LAG_MEAN, unit)
            at("s", here + LAG_SQUARE, unit)
            at("i", here + LAG_INVERSE, unit)
            if l < LAST and unit not in GPSIMD_NORMALISES:
                at("h", here + LAG_SHIFT, unit)
            if l == 0:
                at("t", here - LAG_TURN[grp], rt)
                at("g", here - LAG_GROUP[grp], rt)
                at("q", here - LAG_QUANT[grp], rt)
            if unit in wide_rows:
                at("w", here - LAG_ADD_V, wide_rows[unit])
            if unit in VECTOR_ADDS:
                at("v", here - LAG_ADD_V, unit)
            else:
                at("a", here - LAG_ADD_G, unit)
            if l < LAST:
                at("n", here + LAG_NORMALISE, unit)
            else:
                at("r", here + LAG_CENTRE, unit)
        for l in range(BRANCHES):
            at("f", SPREAD_AT[l], l)
        at("k", COLUMNS_AT, 0)
        stage = {"t": turn_h, "g": group_h, "q": quantise_h, "w": spread_wide, "v": add_bias, "a": add_bias, "m": mean, "s": square,
                 "i": inverse_std, "h": make_shift, "n": normalise, "r": centre_and_gain, "f": spread_bias}
        for step in range(last_step + 1):
            for key in ORDER:
                for what in plan.get((step, key), []):
                    if key == "p":
                        for half in range(HALVES):
                            product(what, half)
                    elif key in "cd":
                        collect(what, "cd".index(key))
                    elif key == "k":
                        vectors_to_columns()
                    else:
                        stage[key](what)
                if key == "b":
                    for job in back.get(step, []):
                        if job[0] == "gain":
                            gain(job[1], job[2])
                        else:
                            finish(job[1], job[2])
